import numpy as np
import ml_dtypes


def mxq(x, axis, fmt="e4m3"):
    dtype, down = {"e4m3": (ml_dtypes.float8_e4m3fn, 7), "e5m2": (ml_dtypes.float8_e5m2, 14)}[fmt]
    v = np.moveaxis(np.asarray(x, np.float32).astype(ml_dtypes.bfloat16).astype(np.float64), axis, -1)
    blocks = v.reshape(v.shape[:-1] + (-1, 32))
    amax = np.abs(blocks).max(-1, keepdims=True)
    byte = np.maximum(np.where(amax > 0, np.frexp(amax)[1] - 1 + 127, 0) - down, 1)
    scale = np.exp2(byte - 127.0)
    codes = (blocks / scale).astype(np.float32).astype(dtype).astype(np.float64)
    return np.moveaxis((codes * scale).reshape(v.shape), -1, axis)


WIDE = False


def mx_kscale(k):
    if not WIDE:
        return np.ones(k)
    levels = np.array([10, -10, 5, -5, 0])
    a = np.random.permutation(np.resize(levels, k // 512 * 4)).reshape(k // 512, 4)
    idx = np.arange(k)
    return np.exp2(a[idx // 512, idx % 128 // 32])


BF16 = ml_dtypes.bfloat16


def bf(x):
    return np.asarray(x, np.float32).astype(BF16)


def f64(x):
    return np.asarray(x).astype(np.float64)


N, V, E1, E2, C, T, EMB = 1024, 4096, 1024, 1024, 128, 512, 1024
BN_EPS = 1e-5


def softplus(v):
    return np.log(1.0 + np.exp(v))


def bn(x, gamma, beta):
    m = x.mean(0)
    v = x.var(0)
    return (x - m) / np.sqrt(v + BN_EPS) * gamma + beta


def setup_inputs():
    s = mx_kscale(E1)
    return {"en1": bf(softplus(np.random.standard_normal((N, E1))) * s),
            "eps": bf(np.random.standard_normal((N, C))),
            "W2": bf(np.random.standard_normal((E2, E1)) / np.sqrt(E1) / s[None, :]),
            "b2": bf(np.random.standard_normal(E2) * 0.3),
            "Wm": bf(np.random.standard_normal((C, E2)) / np.sqrt(E2)),
            "Wv": bf(np.random.standard_normal((C, E2)) / np.sqrt(E2)),
            "gm": bf(0.5 * (1.0 + 0.1 * np.random.standard_normal(C))),
            "betam": bf(np.random.standard_normal(C) * 0.1),
            "gv": bf(0.5 * (1.0 + 0.1 * np.random.standard_normal(C))),
            "betav": bf(-1.5 + 0.1 * np.random.standard_normal(C))}


def reference(en1, eps, W2, b2, Wm, Wv, gm, betam, gv, betav):
    en2 = softplus((mxq(f64(en1), 1, "e4m3") @ mxq(f64(W2), 1, "e4m3").T) + f64(b2))
    en2q = mxq(en2, 1, "e4m3")
    posterior_mean = bn(en2q @ mxq(f64(Wm), 1, "e4m3").T, f64(gm), f64(betam))
    posterior_logvar = bn(en2q @ mxq(f64(Wv), 1, "e4m3").T, f64(gv), f64(betav))
    posterior_var = np.exp(posterior_logvar)
    return posterior_mean + np.sqrt(posterior_var) * f64(eps)

@@ -1,0 +1,277 @@
+from contextlib import ExitStack
+
+import concourse.masks as masks
+import concourse.mybir as mybir
+
+BF16 = mybir.dt.bfloat16
+F32 = mybir.dt.float32
+U32 = mybir.dt.uint32
+U8 = mybir.dt.uint8
+FP8X4 = mybir.dt.float8_e4m3fn_x4
+ACT = mybir.ActivationFunctionType
+ALU = mybir.AluOpType
+
+P = 128
+PACK = 4
+K_PASS = P * PACK
+ROWS = 1024
+K = 1024
+C = 128
+PASSES = K // K_PASS
+PAIRS = PACK // 2
+ROW_TILES = ROWS // P
+CHUNK_TILES = 2
+CHUNK = CHUNK_TILES * P
+CHUNKS = ROWS // CHUNK
+HALF = 512
+HALVES = ROWS // HALF
+HALF_CHUNKS = HALF // CHUNK
+RUN = 4
+SCALAR_SHARE = 4
+AHEAD = 5
+BN_EPS = 1e-5
+MEAN, LOGVAR = 0, 1
+
+FLOPS = 2 * ROWS * K * K + 2 * 2 * ROWS * K * C
+
+
+def tile_model_pa_kernel(tc, en1, eps, W2, b2, Wm, Wv, gm, betam, gv, betav, out):
+    nc = tc.nc
+    with ExitStack() as ctx:
+        const = ctx.enter_context(tc.tile_pool(name="const", bufs=1))
+        raw = ctx.enter_context(tc.tile_pool(name="raw", bufs=1))
+        keep = ctx.enter_context(tc.tile_pool(name="keep", bufs=1))
+        stage = ctx.enter_context(tc.tile_pool(name="stage", bufs=3))
+        tail = ctx.enter_context(tc.tile_pool(name="tail", bufs=2))
+        flip_psum = ctx.enter_context(tc.psum_pool(name="flip_psum", bufs=4))
+        acc_psum = ctx.enter_context(tc.psum_pool(name="acc_psum", bufs=4))
+        ctx.enter_context(tc.manual_schedule())
+
+        en1_rows = en1.rearrange("(p r) k -> p r k", r=ROW_TILES)
+        eps_rows = eps.rearrange("(p r) c -> p r c", r=ROW_TILES)
+        out_rows = out.rearrange("(p r) c -> p r c", r=ROW_TILES)
+        w2_rows = W2.rearrange("(g p t) k -> p g t k", p=P, t=PACK)
+        b2_cols = b2.rearrange("(g p t) -> p g t", p=P, t=PACK)
+
+        x_codes = [keep.tile([P, PASSES, HALF], U32, name="x_codes%d" % h, align_bytes=64) for h in range(HALVES)]
+        x_scales = [keep.tile([P, PASSES, HALF], U8, name="x_scales%d" % h, align_bytes=64) for h in range(HALVES)]
+        w_codes = [keep.tile([P, PASSES, CHUNK], U32, name="w_codes%d" % c, align_bytes=64) for c in range(CHUNKS)]
+        w_scales = [keep.tile([P, PASSES, CHUNK], U8, name="w_scales%d" % c, align_bytes=64) for c in range(CHUNKS)]
+        exp_v = [keep.tile([P, PASSES * PACK, HALF], F32, name="exp_v%d" % h) for h in range(HALVES)]
+
+        def x_chunk(c):
+            h, j = divmod(c, HALF_CHUNKS)
+            cols = slice(j * CHUNK, (j + 1) * CHUNK)
+            return (en1_rows[:, c * CHUNK_TILES : (c + 1) * CHUNK_TILES, :], x_codes[h][:, :, cols], x_scales[h][:, :, cols])
+
+        def w_chunk(c):
+            g, j = divmod(c, PACK // CHUNK_TILES)
+            return (w2_rows[:, g, j * CHUNK_TILES : (j + 1) * CHUNK_TILES, :], w_codes[c][:], w_scales[c][:])
+
+        chunks = [x_chunk(c) for c in range(HALF_CHUNKS)]
+        chunks.extend([w_chunk(c) for c in range(CHUNKS)])
+        chunks.extend([x_chunk(c) for c in range(HALF_CHUNKS, CHUNKS)])
+
+        b2_bf = const.tile([P, PASSES, PACK], BF16)
+        with nc.allow_non_contiguous_dma(reason="8 bytes of b2 to a partition and pass"):
+            nc.scalar.dma_start(out=b2_bf[:], in_=b2_cols)
+        chunk_raw = [raw.tile([P, CHUNK_TILES, K], BF16, name="chunk_raw%d" % n) for n in range(len(chunks))]
+        for n in range(len(chunks)):
+            nc.sync.dma_start(out=chunk_raw[n][:], in_=chunks[n][0])
+        wm_raw = raw.tile([P, K], BF16)
+        wv_raw = raw.tile([P, K], BF16)
+        eps_raw = raw.tile([P, ROW_TILES, C], BF16)
+        nc.sync.dma_start(out=wm_raw[:], in_=Wm)
+        nc.sync.dma_start(out=wv_raw[:], in_=Wv)
+        nc.sync.dma_start(out=eps_raw[:], in_=eps_rows)
+        gm_bf = const.tile([P, 1], BF16)
+        gv_bf = const.tile([P, 1], BF16)
+        betam_bf = const.tile([P, 1], BF16)
+        betav_bf = const.tile([P, 1], BF16)
+        with nc.allow_non_contiguous_dma(reason="one element of a norm's vector to a partition"):
+            nc.sync.dma_start(out=gm_bf[:], in_=gm.rearrange("(p o) -> p o", o=1))
+            nc.sync.dma_start(out=gv_bf[:], in_=gv.rearrange("(p o) -> p o", o=1))
+            nc.sync.dma_start(out=betam_bf[:], in_=betam.rearrange("(p o) -> p o", o=1))
+            nc.sync.dma_start(out=betav_bf[:], in_=betav.rearrange("(p o) -> p o", o=1))
+
+        ident_f32 = const.tile([P, P], F32)
+        masks.make_identity(nc, ident_f32[:])
+        ident_bf = const.tile([P, P], BF16)
+        masks.make_identity(nc, ident_bf[:])
+        one = const.tile([P, 1], F32)
+        nc.vector.memset(one[:], 1.0)
+        neg_half = const.tile([P, 2], F32)
+        nc.vector.memset(neg_half[:], -0.5)
+        b2_f32 = const.tile([P, PASSES * PACK], F32)
+        nc.vector.tensor_copy(out=b2_f32[:], in_=b2_bf[:].rearrange("p g t -> p (g t)"))
+
+        def prepare(n):
+            rows, codes, scales = chunk_raw[n], chunks[n][1], chunks[n][2]
+            grouped = stage.tile([P, PASSES * CHUNK * PACK], BF16, tag="grouped", align_bytes=64)
+            grouped_words = grouped[:].bitcast(F32).rearrange("p (g r u) -> p g r u", g=PASSES, u=PAIRS)
+            for i in range(CHUNK_TILES):
+                words = rows[:, i, :].bitcast(F32)
+                flipped = flip_psum.tile([P, PASSES, PAIRS, P], F32, tag="flip")
+                for g in range(PASSES):
+                    for u in range(PAIRS):
+                        j = g * PAIRS + u
+                        nc.tensor.transpose(flipped[:, g, u, :], words[:, j * P : (j + 1) * P], ident_f32[:])
+                dst = grouped_words[:, :, i * P : (i + 1) * P, :]
+                src = flipped[:].rearrange("p g u r -> p g r u")
+                if (n * CHUNK_TILES + i) % SCALAR_SHARE == SCALAR_SHARE - 1:
+                    nc.scalar.copy(out=dst, in_=src)
+                else:
+                    nc.vector.tensor_copy(out=dst, in_=src)
+            width = CHUNK * PACK
+            for g in range(PASSES):
+                nc.vector.quantize_mx(
+                    out=codes[:, g, :].bitcast(FP8X4),
+                    scales=scales[:, g, :],
+                    in_=grouped[:, g * width : (g + 1) * width],
+                )
+
+        def multiply(c, h):
+            for i in range(CHUNK_TILES):
+                m = c * CHUNK_TILES + i
+                m_cols = slice(i * P, (i + 1) * P)
+                acc = acc_psum.tile([P, HALF], F32, tag="acc")
+                for g in range(PASSES):
+                    nc.tensor.matmul_mx(
+                        out=acc[:],
+                        lhsT=w_codes[c][:, g, m_cols].bitcast(FP8X4),
+                        lhsT_scale=w_scales[c][:, g, m_cols],
+                        rhs=x_codes[h][:, g, :].bitcast(FP8X4),
+                        rhs_scale=x_scales[h][:, g, :],
+                        start=(g == 0),
+                        stop=(g == PASSES - 1),
+                    )
+                nc.scalar.activation(out=exp_v[h][:, m, :], in_=acc[:], func=ACT.Exp, bias=b2_f32[:, m : m + 1], scale=1.0)
+
+        for n in range(AHEAD):
+            prepare(n)
+        for c in range(CHUNKS):
+            multiply(c, 0)
+            if AHEAD + c < len(chunks):
+                prepare(AHEAD + c)
+        for c in range(CHUNKS):
+            multiply(c, 1)
+
+        head_grouped = keep.tile([P, 2 * PASSES * C * PACK], BF16, align_bytes=64)
+        head_words = head_grouped[:].bitcast(F32).rearrange("p (s g c u) -> p s g c u", s=2, g=PASSES, u=PAIRS)
+        head_codes = keep.tile([P, 2, PASSES, C], U32, align_bytes=64)
+        head_scales = keep.tile([P, 2, PASSES, C], U8, align_bytes=64)
+        for s, rows in ((MEAN, wm_raw), (LOGVAR, wv_raw)):
+            words = rows[:].bitcast(F32)
+            flipped = flip_psum.tile([P, PASSES, PAIRS, P], F32, tag="flip")
+            for g in range(PASSES):
+                for u in range(PAIRS):
+                    first = g * PAIRS * P + u
+                    nc.tensor.transpose(flipped[:, g, u, :], words[:, first : (g + 1) * PAIRS * P : PAIRS], ident_f32[:])
+            nc.vector.tensor_copy(out=head_words[:, s, :, :, :], in_=flipped[:].rearrange("p g u c -> p g c u"))
+        nc.vector.quantize_mx(
+            out=head_codes[:].rearrange("p s g c -> p (s g c)").bitcast(FP8X4),
+            scales=head_scales[:].rearrange("p s g c -> p (s g c)"),
+            in_=head_grouped[:],
+        )
+
+        eps_flipped = flip_psum.tile([P, ROW_TILES, P], BF16, tag="flip")
+        for r in range(ROW_TILES):
+            nc.tensor.transpose(eps_flipped[:, r, :], eps_raw[:, r, :], ident_bf[:])
+        eps_t = keep.tile([P, ROW_TILES, P], BF16)
+        nc.vector.tensor_copy(out=eps_t[:], in_=eps_flipped[:])
+
+        gamma = const.tile([P, 2], F32)
+        beta = const.tile([P, 2], F32)
+        nc.vector.tensor_copy(out=gamma[:, MEAN : MEAN + 1], in_=gm_bf[:])
+        nc.vector.tensor_copy(out=beta[:, MEAN : MEAN + 1], in_=betam_bf[:])
+        nc.vector.tensor_scalar(out=gamma[:, LOGVAR : LOGVAR + 1], in0=gv_bf[:], scalar1=0.5, scalar2=None, op0=ALU.mult)
+        nc.vector.tensor_scalar(out=beta[:, LOGVAR : LOGVAR + 1], in0=betav_bf[:], scalar1=0.5, scalar2=None, op0=ALU.mult)
+
+        hidden = [[acc_psum.tile([P, HALF], F32, tag="acc", name="hidden%d%d" % (s, h)) for h in range(HALVES)] for s in range(2)]
+        stats = keep.tile([P, 2, CHUNKS, 6], F32)
+        table_scratch = const.tile([P, 1], F32)
+        for x in range(CHUNKS):
+            h, j = divmod(x, HALF_CHUNKS)
+            cols = slice(j * CHUNK, (j + 1) * CHUNK)
+            for g in range(PASSES):
+                en2 = stage.tile([P, CHUNK * PACK], BF16, tag="en2", align_bytes=64)
+                en2_codes = stage.tile([P, CHUNK], U32, tag="en2_codes", align_bytes=64)
+                en2_scales = stage.tile([P, CHUNK], U8, tag="en2_scales", align_bytes=64)
+                nc.scalar.activation(
+                    out=en2[:].rearrange("p (c i t) -> p c t i", i=RUN, t=PACK),
+                    in_=exp_v[h][:, g * PACK : (g + 1) * PACK, cols].rearrange("p t (c i) -> p c t i", i=RUN),
+                    func=ACT.Ln,
+                    bias=one[:],
+                    scale=1.0,
+                )
+                nc.vector.quantize_mx(out=en2_codes[:].bitcast(FP8X4), scales=en2_scales[:], in_=en2[:])
+                for s in (LOGVAR, MEAN):
+                    nc.tensor.matmul_mx(
+                        out=hidden[s][h][:, cols],
+                        lhsT=head_codes[:, s, g, :].bitcast(FP8X4),
+                        lhsT_scale=head_scales[:, s, g, :],
+                        rhs=en2_codes[:].bitcast(FP8X4),
+                        rhs_scale=en2_scales[:],
+                        start=(g == 0),
+                        stop=(g == PASSES - 1),
+                    )
+            for s in (LOGVAR, MEAN):
+                nc.vector.bn_stats(out=stats[:, s, x, :], in_=hidden[s][h][:, cols])
+
+        nc.scalar.activation(out=table_scratch[:], in_=en2[:, 0:1], func=ACT.Exp)
+
+        mean_var = const.tile([P, 2, 2], F32)
+        for s in (LOGVAR, MEAN):
+            nc.vector.bn_aggr(out=mean_var[:, s, :], in_=stats[:, s, :, :].rearrange("p x k -> p (x k)"))
+        var_eps = const.tile([P, 2], F32)
+        nc.vector.tensor_scalar(out=var_eps[:], in0=mean_var[:, :, 1], scalar1=BN_EPS, scalar2=None, op0=ALU.add)
+        rstd = const.tile([P, 2], F32)
+        nc.gpsimd.tensor_tensor(out=rstd[:], in0=var_eps[:], in1=neg_half[:], op=ALU.pow)
+        neg_mean_gamma = const.tile([P, 2], F32)
+        nc.vector.scalar_tensor_tensor(
+            out=neg_mean_gamma[:], in0=mean_var[:, :, 0], scalar=-1.0, in1=gamma[:], op0=ALU.mult, op1=ALU.mult
+        )
+        gain = const.tile([P, 2], F32)
+        nc.vector.tensor_tensor(out=gain[:], in0=rstd[:], in1=gamma[:], op=ALU.mult)
+        shift = const.tile([P, 2], F32)
+        for s in (LOGVAR, MEAN):
+            nc.vector.tensor_scalar(
+                out=shift[:, s : s + 1],
+                in0=neg_mean_gamma[:, s : s + 1],
+                scalar1=rstd[:, s : s + 1],
+                scalar2=beta[:, s : s + 1],
+                op0=ALU.mult,
+                op1=ALU.add,
+            )
+
+        z_t = [tail.tile([P, HALF], F32, name="z_t%d" % h) for h in range(HALVES)]
+        for h in range(HALVES):
+            std = tail.tile([P, HALF], F32, tag="std")
+            nc.scalar.activation(
+                out=std[:], in_=hidden[LOGVAR][h][:], func=ACT.Exp,
+                bias=shift[:, LOGVAR : LOGVAR + 1], scale=gain[:, LOGVAR : LOGVAR + 1],
+            )
+            mean = tail.tile([P, HALF], F32, tag="mean")
+            nc.scalar.activation(
+                out=mean[:], in_=hidden[MEAN][h][:], func=ACT.Identity,
+                bias=shift[:, MEAN : MEAN + 1], scale=gain[:, MEAN : MEAN + 1],
+            )
+            noise = tail.tile([P, HALF], F32, tag="noise")
+            tiles = slice(h * (HALF // P), (h + 1) * (HALF // P))
+            nc.vector.tensor_tensor(out=noise[:], in0=std[:], in1=eps_t[:, tiles, :].rearrange("p r q -> p (r q)"), op=ALU.mult)
+            nc.vector.tensor_tensor(out=z_t[h][:], in0=noise[:], in1=mean[:], op=ALU.add)
+        z_rows = keep.tile([P, ROW_TILES, C], F32)
+        for x in range(CHUNKS):
+            h, j = divmod(x, HALF_CHUNKS)
+            z_flipped = flip_psum.tile([P, CHUNK_TILES, C], F32, tag="flip")
+            for i in range(CHUNK_TILES):
+                first = j * CHUNK + i * P
+                nc.tensor.transpose(z_flipped[:, i, :], z_t[h][:, first : first + P], ident_f32[:])
+            tiles = slice(x * CHUNK_TILES, (x + 1) * CHUNK_TILES)
+            if x % 2 == 0:
+                nc.scalar.copy(out=z_rows[:, tiles, :], in_=z_flipped[:])
+            else:
+                nc.vector.tensor_copy(out=z_rows[:, tiles, :], in_=z_flipped[:])
+            if j == HALF_CHUNKS - 1:
+                tiles = slice(h * (HALF // P), (h + 1) * (HALF // P))
+                nc.sync.dma_start(out=out_rows[:, tiles, :], in_=z_rows[:, tiles, :])

@@ -29,6 +29,7 @@ HALF_CHUNKS = HALF // CHUNK
 RUN = 4
 SCALAR_SHARE = 4
 AHEAD = 5
+WARM_FIRST = 4
 BN_EPS = 1e-5
 MEAN, LOGVAR = 0, 1
 
@@ -98,12 +99,19 @@ def tile_model_pa_kernel(tc, en1, eps, W2, b2, Wm, Wv, gm, betam, gv, betav, out
         masks.make_identity(nc, ident_f32[:])
         ident_bf = const.tile([P, P], BF16)
         masks.make_identity(nc, ident_bf[:])
+        zeros = const.tile([P, HALF], BF16)
+        nc.vector.memset(zeros[:], 0.0)
         one = const.tile([P, 1], F32)
         nc.vector.memset(one[:], 1.0)
         neg_half = const.tile([P, 2], F32)
         nc.vector.memset(neg_half[:], -0.5)
         b2_f32 = const.tile([P, PASSES * PACK], F32)
         nc.vector.tensor_copy(out=b2_f32[:], in_=b2_bf[:].rearrange("p g t -> p (g t)"))
+
+        idle_sums = acc_psum.tile([P, HALF], F32, tag="acc")
+
+        def idle_matmul():
+            nc.tensor.matmul(out=idle_sums[:], lhsT=ident_bf[:], rhs=zeros[:], start=True, stop=True)
 
         def prepare(n):
             rows, codes, scales = chunk_raw[n], chunks[n][1], chunks[n][2]
@@ -147,8 +155,11 @@ def tile_model_pa_kernel(tc, en1, eps, W2, b2, Wm, Wv, gm, betam, gv, betav, out
                     )
                 nc.scalar.activation(out=exp_v[h][:, m, :], in_=acc[:], func=ACT.Exp, bias=b2_f32[:, m : m + 1], scale=1.0)
 
+        for n in range(WARM_FIRST):
+            idle_matmul()
         for n in range(AHEAD):
             prepare(n)
+            idle_matmul()
         for c in range(CHUNKS):
             multiply(c, 0)
             if AHEAD + c < len(chunks):

@@ -27,9 +27,7 @@ HALF = 512
 HALVES = ROWS // HALF
 HALF_CHUNKS = HALF // CHUNK
 RUN = 4
-SCALAR_SHARE = 4
-AHEAD = 5
-WARM_FIRST = 4
+AHEAD = 6
 BN_EPS = 1e-5
 MEAN, LOGVAR = 0, 1
 
@@ -43,7 +41,7 @@ def tile_model_pa_kernel(tc, en1, eps, W2, b2, Wm, Wv, gm, betam, gv, betav, out
         raw = ctx.enter_context(tc.tile_pool(name="raw", bufs=1))
         keep = ctx.enter_context(tc.tile_pool(name="keep", bufs=1))
         stage = ctx.enter_context(tc.tile_pool(name="stage", bufs=3))
-        tail = ctx.enter_context(tc.tile_pool(name="tail", bufs=2))
+        tail = ctx.enter_context(tc.tile_pool(name="tail", bufs=1))
         flip_psum = ctx.enter_context(tc.psum_pool(name="flip_psum", bufs=4))
         acc_psum = ctx.enter_context(tc.psum_pool(name="acc_psum", bufs=4))
         ctx.enter_context(tc.manual_schedule())
@@ -99,26 +97,20 @@ def tile_model_pa_kernel(tc, en1, eps, W2, b2, Wm, Wv, gm, betam, gv, betav, out
         masks.make_identity(nc, ident_f32[:])
         ident_bf = const.tile([P, P], BF16)
         masks.make_identity(nc, ident_bf[:])
-        zeros = const.tile([P, HALF], BF16)
-        nc.vector.memset(zeros[:], 0.0)
         one = const.tile([P, 1], F32)
         nc.vector.memset(one[:], 1.0)
-        neg_half = const.tile([P, 2], F32)
+        neg_half = const.tile([P, 1], F32)
         nc.vector.memset(neg_half[:], -0.5)
         b2_f32 = const.tile([P, PASSES * PACK], F32)
         nc.vector.tensor_copy(out=b2_f32[:], in_=b2_bf[:].rearrange("p g t -> p (g t)"))
 
-        idle_sums = acc_psum.tile([P, HALF], F32, tag="acc")
+        grouped = {}
 
-        def idle_matmul():
-            nc.tensor.matmul(out=idle_sums[:], lhsT=ident_bf[:], rhs=zeros[:], start=True, stop=True)
-
-        def prepare(n):
-            rows, codes, scales = chunk_raw[n], chunks[n][1], chunks[n][2]
-            grouped = stage.tile([P, PASSES * CHUNK * PACK], BF16, tag="grouped", align_bytes=64)
-            grouped_words = grouped[:].bitcast(F32).rearrange("p (g r u) -> p g r u", g=PASSES, u=PAIRS)
+        def flip(n):
+            grouped[n] = stage.tile([P, PASSES * CHUNK * PACK], BF16, tag="grouped", name="grouped%d" % n, align_bytes=64)
+            grouped_words = grouped[n][:].bitcast(F32).rearrange("p (g r u) -> p g r u", g=PASSES, u=PAIRS)
             for i in range(CHUNK_TILES):
-                words = rows[:, i, :].bitcast(F32)
+                words = chunk_raw[n][:, i, :].bitcast(F32)
                 flipped = flip_psum.tile([P, PASSES, PAIRS, P], F32, tag="flip")
                 for g in range(PASSES):
                     for u in range(PAIRS):
@@ -126,16 +118,19 @@ def tile_model_pa_kernel(tc, en1, eps, W2, b2, Wm, Wv, gm, betam, gv, betav, out
                         nc.tensor.transpose(flipped[:, g, u, :], words[:, j * P : (j + 1) * P], ident_f32[:])
                 dst = grouped_words[:, :, i * P : (i + 1) * P, :]
                 src = flipped[:].rearrange("p g u r -> p g r u")
-                if (n * CHUNK_TILES + i) % SCALAR_SHARE == SCALAR_SHARE - 1:
-                    nc.scalar.copy(out=dst, in_=src)
-                else:
+                if i % 2 == 0:
                     nc.vector.tensor_copy(out=dst, in_=src)
+                else:
+                    nc.scalar.copy(out=dst, in_=src)
+
+        def quantise(n):
+            codes, scales = chunks[n][1], chunks[n][2]
             width = CHUNK * PACK
             for g in range(PASSES):
                 nc.vector.quantize_mx(
                     out=codes[:, g, :].bitcast(FP8X4),
                     scales=scales[:, g, :],
-                    in_=grouped[:, g * width : (g + 1) * width],
+                    in_=grouped[n][:, g * width : (g + 1) * width],
                 )
 
         def multiply(c, h):
@@ -155,15 +150,17 @@ def tile_model_pa_kernel(tc, en1, eps, W2, b2, Wm, Wv, gm, betam, gv, betav, out
                     )
                 nc.scalar.activation(out=exp_v[h][:, m, :], in_=acc[:], func=ACT.Exp, bias=b2_f32[:, m : m + 1], scale=1.0)
 
-        for n in range(WARM_FIRST):
-            idle_matmul()
         for n in range(AHEAD):
-            prepare(n)
-            idle_matmul()
+            flip(n)
+            if n > 0:
+                quantise(n - 1)
         for c in range(CHUNKS):
             multiply(c, 0)
-            if AHEAD + c < len(chunks):
-                prepare(AHEAD + c)
+            n = AHEAD + c
+            if n < len(chunks):
+                flip(n)
+            if n <= len(chunks):
+                quantise(n - 1)
         for c in range(CHUNKS):
             multiply(c, 1)
 
@@ -179,17 +176,16 @@ def tile_model_pa_kernel(tc, en1, eps, W2, b2, Wm, Wv, gm, betam, gv, betav, out
                     first = g * PAIRS * P + u
                     nc.tensor.transpose(flipped[:, g, u, :], words[:, first : (g + 1) * PAIRS * P : PAIRS], ident_f32[:])
             nc.vector.tensor_copy(out=head_words[:, s, :, :, :], in_=flipped[:].rearrange("p g u c -> p g c u"))
-        nc.vector.quantize_mx(
-            out=head_codes[:].rearrange("p s g c -> p (s g c)").bitcast(FP8X4),
-            scales=head_scales[:].rearrange("p s g c -> p (s g c)"),
-            in_=head_grouped[:],
-        )
-
         eps_flipped = flip_psum.tile([P, ROW_TILES, P], BF16, tag="flip")
         for r in range(ROW_TILES):
             nc.tensor.transpose(eps_flipped[:, r, :], eps_raw[:, r, :], ident_bf[:])
         eps_t = keep.tile([P, ROW_TILES, P], BF16)
         nc.vector.tensor_copy(out=eps_t[:], in_=eps_flipped[:])
+        nc.vector.quantize_mx(
+            out=head_codes[:].rearrange("p s g c -> p (s g c)").bitcast(FP8X4),
+            scales=head_scales[:].rearrange("p s g c -> p (s g c)"),
+            in_=head_grouped[:],
+        )
 
         gamma = const.tile([P, 2], F32)
         beta = const.tile([P, 2], F32)
@@ -201,6 +197,11 @@ def tile_model_pa_kernel(tc, en1, eps, W2, b2, Wm, Wv, gm, betam, gv, betav, out
         hidden = [[acc_psum.tile([P, HALF], F32, tag="acc", name="hidden%d%d" % (s, h)) for h in range(HALVES)] for s in range(2)]
         stats = keep.tile([P, 2, CHUNKS, 6], F32)
         table_scratch = const.tile([P, 1], F32)
+
+        def statistics(x, s):
+            h, j = divmod(x, HALF_CHUNKS)
+            nc.vector.bn_stats(out=stats[:, s, x, :], in_=hidden[s][h][:, j * CHUNK : (j + 1) * CHUNK])
+
         for x in range(CHUNKS):
             h, j = divmod(x, HALF_CHUNKS)
             cols = slice(j * CHUNK, (j + 1) * CHUNK)
@@ -226,63 +227,59 @@ def tile_model_pa_kernel(tc, en1, eps, W2, b2, Wm, Wv, gm, betam, gv, betav, out
                         start=(g == 0),
                         stop=(g == PASSES - 1),
                     )
-            for s in (LOGVAR, MEAN):
-                nc.vector.bn_stats(out=stats[:, s, x, :], in_=hidden[s][h][:, cols])
-
+            if x > 0:
+                for s in (LOGVAR, MEAN):
+                    statistics(x - 1, s)
         nc.scalar.activation(out=table_scratch[:], in_=en2[:, 0:1], func=ACT.Exp)
 
+        rstd = [const.tile([P, 1], F32, name="rstd%d" % s) for s in range(2)]
         mean_var = const.tile([P, 2, 2], F32)
-        for s in (LOGVAR, MEAN):
-            nc.vector.bn_aggr(out=mean_var[:, s, :], in_=stats[:, s, :, :].rearrange("p x k -> p (x k)"))
         var_eps = const.tile([P, 2], F32)
-        nc.vector.tensor_scalar(out=var_eps[:], in0=mean_var[:, :, 1], scalar1=BN_EPS, scalar2=None, op0=ALU.add)
-        rstd = const.tile([P, 2], F32)
-        nc.gpsimd.tensor_tensor(out=rstd[:], in0=var_eps[:], in1=neg_half[:], op=ALU.pow)
         neg_mean_gamma = const.tile([P, 2], F32)
-        nc.vector.scalar_tensor_tensor(
-            out=neg_mean_gamma[:], in0=mean_var[:, :, 0], scalar=-1.0, in1=gamma[:], op0=ALU.mult, op1=ALU.mult
-        )
         gain = const.tile([P, 2], F32)
-        nc.vector.tensor_tensor(out=gain[:], in0=rstd[:], in1=gamma[:], op=ALU.mult)
         shift = const.tile([P, 2], F32)
         for s in (LOGVAR, MEAN):
+            col = slice(s, s + 1)
+            statistics(CHUNKS - 1, s)
+            nc.vector.bn_aggr(out=mean_var[:, s, :], in_=stats[:, s, :, :].rearrange("p x k -> p (x k)"))
+            nc.vector.tensor_scalar(out=var_eps[:, col], in0=mean_var[:, s, 1:2], scalar1=BN_EPS, scalar2=None, op0=ALU.add)
+            nc.gpsimd.tensor_tensor(out=rstd[s][:], in0=var_eps[:, col], in1=neg_half[:], op=ALU.pow)
+            nc.vector.scalar_tensor_tensor(
+                out=neg_mean_gamma[:, col], in0=mean_var[:, s, 0:1], scalar=-1.0, in1=gamma[:, col], op0=ALU.mult, op1=ALU.mult
+            )
+        for s in (LOGVAR, MEAN):
+            col = slice(s, s + 1)
+            nc.vector.tensor_tensor(out=gain[:, col], in0=rstd[s][:], in1=gamma[:, col], op=ALU.mult)
             nc.vector.tensor_scalar(
-                out=shift[:, s : s + 1],
-                in0=neg_mean_gamma[:, s : s + 1],
-                scalar1=rstd[:, s : s + 1],
-                scalar2=beta[:, s : s + 1],
-                op0=ALU.mult,
-                op1=ALU.add,
+                out=shift[:, col], in0=neg_mean_gamma[:, col], scalar1=rstd[s][:], scalar2=beta[:, col], op0=ALU.mult, op1=ALU.add
             )
 
+        std = [tail.tile([P, HALF], F32, name="std%d" % h) for h in range(HALVES)]
+        mean = [tail.tile([P, HALF], F32, name="mean%d" % h) for h in range(HALVES)]
+        noise = [tail.tile([P, HALF], F32, name="noise%d" % h) for h in range(HALVES)]
         z_t = [tail.tile([P, HALF], F32, name="z_t%d" % h) for h in range(HALVES)]
         for h in range(HALVES):
-            std = tail.tile([P, HALF], F32, tag="std")
             nc.scalar.activation(
-                out=std[:], in_=hidden[LOGVAR][h][:], func=ACT.Exp,
+                out=std[h][:], in_=hidden[LOGVAR][h][:], func=ACT.Exp,
                 bias=shift[:, LOGVAR : LOGVAR + 1], scale=gain[:, LOGVAR : LOGVAR + 1],
             )
-            mean = tail.tile([P, HALF], F32, tag="mean")
+        for h in range(HALVES):
             nc.scalar.activation(
-                out=mean[:], in_=hidden[MEAN][h][:], func=ACT.Identity,
+                out=mean[h][:], in_=hidden[MEAN][h][:], func=ACT.Identity,
                 bias=shift[:, MEAN : MEAN + 1], scale=gain[:, MEAN : MEAN + 1],
             )
-            noise = tail.tile([P, HALF], F32, tag="noise")
+        for h in range(HALVES):
             tiles = slice(h * (HALF // P), (h + 1) * (HALF // P))
-            nc.vector.tensor_tensor(out=noise[:], in0=std[:], in1=eps_t[:, tiles, :].rearrange("p r q -> p (r q)"), op=ALU.mult)
-            nc.vector.tensor_tensor(out=z_t[h][:], in0=noise[:], in1=mean[:], op=ALU.add)
+            nc.vector.tensor_tensor(out=noise[h][:], in0=std[h][:], in1=eps_t[:, tiles, :].rearrange("p r q -> p (r q)"), op=ALU.mult)
         z_rows = keep.tile([P, ROW_TILES, C], F32)
-        for x in range(CHUNKS):
-            h, j = divmod(x, HALF_CHUNKS)
-            z_flipped = flip_psum.tile([P, CHUNK_TILES, C], F32, tag="flip")
-            for i in range(CHUNK_TILES):
-                first = j * CHUNK + i * P
-                nc.tensor.transpose(z_flipped[:, i, :], z_t[h][:, first : first + P], ident_f32[:])
-            tiles = slice(x * CHUNK_TILES, (x + 1) * CHUNK_TILES)
-            if x % 2 == 0:
-                nc.scalar.copy(out=z_rows[:, tiles, :], in_=z_flipped[:])
-            else:
-                nc.vector.tensor_copy(out=z_rows[:, tiles, :], in_=z_flipped[:])
-            if j == HALF_CHUNKS - 1:
-                tiles = slice(h * (HALF // P), (h + 1) * (HALF // P))
-                nc.sync.dma_start(out=out_rows[:, tiles, :], in_=z_rows[:, tiles, :])
+        for h in range(HALVES):
+            nc.vector.tensor_tensor(out=z_t[h][:], in0=noise[h][:], in1=mean[h][:], op=ALU.add)
+            for j in range(HALF_CHUNKS):
+                x = h * HALF_CHUNKS + j
+                z_flipped = flip_psum.tile([P, CHUNK_TILES, C], F32, tag="flip")
+                for i in range(CHUNK_TILES):
+                    first = j * CHUNK + i * P
+                    nc.tensor.transpose(z_flipped[:, i, :], z_t[h][:, first : first + P], ident_f32[:])
+                nc.scalar.copy(out=z_rows[:, x * CHUNK_TILES : (x + 1) * CHUNK_TILES, :], in_=z_flipped[:])
+            tiles = slice(h * (HALF // P), (h + 1) * (HALF // P))
+            nc.sync.dma_start(out=out_rows[:, tiles, :], in_=z_rows[:, tiles, :])

@@ -209,12 +209,17 @@ def tile_model_pa_kernel(tc, en1, eps, W2, b2, Wm, Wv, gm, betam, gv, betav, out
                 en2 = stage.tile([P, CHUNK * PACK], BF16, tag="en2", align_bytes=64)
                 en2_codes = stage.tile([P, CHUNK], U32, tag="en2_codes", align_bytes=64)
                 en2_scales = stage.tile([P, CHUNK], U8, tag="en2_scales", align_bytes=64)
+                en2_rows = stage.tile([P, PACK, CHUNK], BF16, tag="en2_rows")
                 nc.scalar.activation(
-                    out=en2[:].rearrange("p (c i t) -> p c t i", i=RUN, t=PACK),
-                    in_=exp_v[h][:, g * PACK : (g + 1) * PACK, cols].rearrange("p t (c i) -> p c t i", i=RUN),
+                    out=en2_rows[:],
+                    in_=exp_v[h][:, g * PACK : (g + 1) * PACK, cols],
                     func=ACT.Ln,
                     bias=one[:],
                     scale=1.0,
+                )
+                nc.vector.tensor_copy(
+                    out=en2[:].rearrange("p (c i t) -> p c t i", i=RUN, t=PACK),
+                    in_=en2_rows[:].rearrange("p t (c i) -> p c t i", i=RUN),
                 )
                 nc.vector.quantize_mx(out=en2_codes[:].bitcast(FP8X4), scales=en2_scales[:], in_=en2[:])
                 for s in (LOGVAR, MEAN):
@@ -230,7 +235,7 @@ def tile_model_pa_kernel(tc, en1, eps, W2, b2, Wm, Wv, gm, betam, gv, betav, out
             if x > 0:
                 for s in (LOGVAR, MEAN):
                     statistics(x - 1, s)
-        nc.scalar.activation(out=table_scratch[:], in_=en2[:, 0:1], func=ACT.Exp)
+        nc.scalar.activation(out=table_scratch[:], in_=en2_rows[:, 0, 0:1], func=ACT.Exp)
 
         rstd = [const.tile([P, 1], F32, name="rstd%d" % s) for s in range(2)]
         mean_var = const.tile([P, 2, 2], F32)

@@ -13,12 +13,12 @@ ALU = mybir.AluOpType
 
 P = 128
 PACK = 4
+PAIRS = PACK // 2
 K_PASS = P * PACK
 ROWS = 1024
 K = 1024
 C = 128
 PASSES = K // K_PASS
-PAIRS = PACK // 2
 ROW_TILES = ROWS // P
 CHUNK_TILES = 2
 CHUNK = CHUNK_TILES * P
@@ -27,8 +27,11 @@ HALF = 512
 HALVES = ROWS // HALF
 HALF_CHUNKS = HALF // CHUNK
 RUN = 4
-AHEAD = 6
+AHEAD = HALF_CHUNKS + CHUNKS
+BN_STATS_DIM = 6
+BN_AGGR_DIM = 2
 BN_EPS = 1e-5
+HEADS = 2
 MEAN, LOGVAR = 0, 1
 
 FLOPS = 2 * ROWS * K * K + 2 * 2 * ROWS * K * C
@@ -64,8 +67,8 @@ def tile_model_pa_kernel(tc, en1, eps, W2, b2, Wm, Wv, gm, betam, gv, betav, out
             return (en1_rows[:, c * CHUNK_TILES : (c + 1) * CHUNK_TILES, :], x_codes[h][:, :, cols], x_scales[h][:, :, cols])
 
         def w_chunk(c):
-            g, j = divmod(c, PACK // CHUNK_TILES)
-            return (w2_rows[:, g, j * CHUNK_TILES : (j + 1) * CHUNK_TILES, :], w_codes[c][:], w_scales[c][:])
+            g, pair = divmod(c, PACK // CHUNK_TILES)
+            return (w2_rows[:, g, pair * CHUNK_TILES : (pair + 1) * CHUNK_TILES, :], w_codes[c][:], w_scales[c][:])
 
         chunks = [x_chunk(c) for c in range(HALF_CHUNKS)]
         chunks.extend([w_chunk(c) for c in range(CHUNKS)])
@@ -114,8 +117,8 @@ def tile_model_pa_kernel(tc, en1, eps, W2, b2, Wm, Wv, gm, betam, gv, betav, out
                 flipped = flip_psum.tile([P, PASSES, PAIRS, P], F32, tag="flip")
                 for g in range(PASSES):
                     for u in range(PAIRS):
-                        j = g * PAIRS + u
-                        nc.tensor.transpose(flipped[:, g, u, :], words[:, j * P : (j + 1) * P], ident_f32[:])
+                        block = g * PAIRS + u
+                        nc.tensor.transpose(flipped[:, g, u, :], words[:, block * P : (block + 1) * P], ident_f32[:])
                 dst = grouped_words[:, :, i * P : (i + 1) * P, :]
                 src = flipped[:].rearrange("p g u r -> p g r u")
                 if i % 2 == 0:
@@ -164,10 +167,10 @@ def tile_model_pa_kernel(tc, en1, eps, W2, b2, Wm, Wv, gm, betam, gv, betav, out
         for c in range(CHUNKS):
             multiply(c, 1)
 
-        head_grouped = keep.tile([P, 2 * PASSES * C * PACK], BF16, align_bytes=64)
-        head_words = head_grouped[:].bitcast(F32).rearrange("p (s g c u) -> p s g c u", s=2, g=PASSES, u=PAIRS)
-        head_codes = keep.tile([P, 2, PASSES, C], U32, align_bytes=64)
-        head_scales = keep.tile([P, 2, PASSES, C], U8, align_bytes=64)
+        head_grouped = keep.tile([P, HEADS * PASSES * C * PACK], BF16, align_bytes=64)
+        head_words = head_grouped[:].bitcast(F32).rearrange("p (s g c u) -> p s g c u", s=HEADS, g=PASSES, u=PAIRS)
+        head_codes = keep.tile([P, HEADS, PASSES, C], U32, align_bytes=64)
+        head_scales = keep.tile([P, HEADS, PASSES, C], U8, align_bytes=64)
         for s, rows in ((MEAN, wm_raw), (LOGVAR, wv_raw)):
             words = rows[:].bitcast(F32)
             flipped = flip_psum.tile([P, PASSES, PAIRS, P], F32, tag="flip")
@@ -187,39 +190,34 @@ def tile_model_pa_kernel(tc, en1, eps, W2, b2, Wm, Wv, gm, betam, gv, betav, out
             in_=head_grouped[:],
         )
 
-        gamma = const.tile([P, 2], F32)
-        beta = const.tile([P, 2], F32)
+        gamma = const.tile([P, HEADS], F32)
+        beta = const.tile([P, HEADS], F32)
         nc.vector.tensor_copy(out=gamma[:, MEAN : MEAN + 1], in_=gm_bf[:])
         nc.vector.tensor_copy(out=beta[:, MEAN : MEAN + 1], in_=betam_bf[:])
         nc.vector.tensor_scalar(out=gamma[:, LOGVAR : LOGVAR + 1], in0=gv_bf[:], scalar1=0.5, scalar2=None, op0=ALU.mult)
         nc.vector.tensor_scalar(out=beta[:, LOGVAR : LOGVAR + 1], in0=betav_bf[:], scalar1=0.5, scalar2=None, op0=ALU.mult)
 
-        hidden = [[acc_psum.tile([P, HALF], F32, tag="acc", name="hidden%d%d" % (s, h)) for h in range(HALVES)] for s in range(2)]
-        stats = keep.tile([P, 2, CHUNKS, 6], F32)
+        hidden = [[acc_psum.tile([P, HALF], F32, tag="acc", name="hidden%d%d" % (s, h)) for h in range(HALVES)] for s in range(HEADS)]
+        stats = keep.tile([P, HEADS, CHUNKS, BN_STATS_DIM], F32)
         table_scratch = const.tile([P, 1], F32)
 
-        def statistics(x, s):
-            h, j = divmod(x, HALF_CHUNKS)
-            nc.vector.bn_stats(out=stats[:, s, x, :], in_=hidden[s][h][:, j * CHUNK : (j + 1) * CHUNK])
+        def statistics(c, s):
+            h, j = divmod(c, HALF_CHUNKS)
+            nc.vector.bn_stats(out=stats[:, s, c, :], in_=hidden[s][h][:, j * CHUNK : (j + 1) * CHUNK])
 
-        for x in range(CHUNKS):
-            h, j = divmod(x, HALF_CHUNKS)
+        for c in range(CHUNKS):
+            h, j = divmod(c, HALF_CHUNKS)
             cols = slice(j * CHUNK, (j + 1) * CHUNK)
             for g in range(PASSES):
                 en2 = stage.tile([P, CHUNK * PACK], BF16, tag="en2", align_bytes=64)
                 en2_codes = stage.tile([P, CHUNK], U32, tag="en2_codes", align_bytes=64)
                 en2_scales = stage.tile([P, CHUNK], U8, tag="en2_scales", align_bytes=64)
-                en2_rows = stage.tile([P, PACK, CHUNK], BF16, tag="en2_rows")
                 nc.scalar.activation(
-                    out=en2_rows[:],
-                    in_=exp_v[h][:, g * PACK : (g + 1) * PACK, cols],
+                    out=en2[:].rearrange("p (a i t) -> p a t i", i=RUN, t=PACK),
+                    in_=exp_v[h][:, g * PACK : (g + 1) * PACK, cols].rearrange("p t (a i) -> p a t i", i=RUN),
                     func=ACT.Ln,
                     bias=one[:],
                     scale=1.0,
-                )
-                nc.vector.tensor_copy(
-                    out=en2[:].rearrange("p (c i t) -> p c t i", i=RUN, t=PACK),
-                    in_=en2_rows[:].rearrange("p t (c i) -> p c t i", i=RUN),
                 )
                 nc.vector.quantize_mx(out=en2_codes[:].bitcast(FP8X4), scales=en2_scales[:], in_=en2[:])
                 for s in (LOGVAR, MEAN):
@@ -232,21 +230,21 @@ def tile_model_pa_kernel(tc, en1, eps, W2, b2, Wm, Wv, gm, betam, gv, betav, out
                         start=(g == 0),
                         stop=(g == PASSES - 1),
                     )
-            if x > 0:
+            if c > 0:
                 for s in (LOGVAR, MEAN):
-                    statistics(x - 1, s)
-        nc.scalar.activation(out=table_scratch[:], in_=en2_rows[:, 0, 0:1], func=ACT.Exp)
+                    statistics(c - 1, s)
+        nc.scalar.activation(out=table_scratch[:], in_=en2[:, 0:1], func=ACT.Exp)
 
-        rstd = [const.tile([P, 1], F32, name="rstd%d" % s) for s in range(2)]
-        mean_var = const.tile([P, 2, 2], F32)
-        var_eps = const.tile([P, 2], F32)
-        neg_mean_gamma = const.tile([P, 2], F32)
-        gain = const.tile([P, 2], F32)
-        shift = const.tile([P, 2], F32)
+        rstd = [const.tile([P, 1], F32, name="rstd%d" % s) for s in range(HEADS)]
+        mean_var = const.tile([P, HEADS, BN_AGGR_DIM], F32)
+        var_eps = const.tile([P, HEADS], F32)
+        neg_mean_gamma = const.tile([P, HEADS], F32)
+        gain = const.tile([P, HEADS], F32)
+        shift = const.tile([P, HEADS], F32)
         for s in (LOGVAR, MEAN):
             col = slice(s, s + 1)
             statistics(CHUNKS - 1, s)
-            nc.vector.bn_aggr(out=mean_var[:, s, :], in_=stats[:, s, :, :].rearrange("p x k -> p (x k)"))
+            nc.vector.bn_aggr(out=mean_var[:, s, :], in_=stats[:, s, :, :].rearrange("p c k -> p (c k)"))
             nc.vector.tensor_scalar(out=var_eps[:, col], in0=mean_var[:, s, 1:2], scalar1=BN_EPS, scalar2=None, op0=ALU.add)
             nc.gpsimd.tensor_tensor(out=rstd[s][:], in0=var_eps[:, col], in1=neg_half[:], op=ALU.pow)
             nc.vector.scalar_tensor_tensor(
@@ -262,7 +260,6 @@ def tile_model_pa_kernel(tc, en1, eps, W2, b2, Wm, Wv, gm, betam, gv, betav, out
         std = [tail.tile([P, HALF], F32, name="std%d" % h) for h in range(HALVES)]
         mean = [tail.tile([P, HALF], F32, name="mean%d" % h) for h in range(HALVES)]
         noise = [tail.tile([P, HALF], F32, name="noise%d" % h) for h in range(HALVES)]
-        z_t = [tail.tile([P, HALF], F32, name="z_t%d" % h) for h in range(HALVES)]
         for h in range(HALVES):
             nc.scalar.activation(
                 out=std[h][:], in_=hidden[LOGVAR][h][:], func=ACT.Exp,
@@ -277,14 +274,14 @@ def tile_model_pa_kernel(tc, en1, eps, W2, b2, Wm, Wv, gm, betam, gv, betav, out
             tiles = slice(h * (HALF // P), (h + 1) * (HALF // P))
             nc.vector.tensor_tensor(out=noise[h][:], in0=std[h][:], in1=eps_t[:, tiles, :].rearrange("p r q -> p (r q)"), op=ALU.mult)
         z_rows = keep.tile([P, ROW_TILES, C], F32)
-        for h in range(HALVES):
-            nc.vector.tensor_tensor(out=z_t[h][:], in0=noise[h][:], in1=mean[h][:], op=ALU.add)
-            for j in range(HALF_CHUNKS):
-                x = h * HALF_CHUNKS + j
-                z_flipped = flip_psum.tile([P, CHUNK_TILES, C], F32, tag="flip")
-                for i in range(CHUNK_TILES):
-                    first = j * CHUNK + i * P
-                    nc.tensor.transpose(z_flipped[:, i, :], z_t[h][:, first : first + P], ident_f32[:])
-                nc.scalar.copy(out=z_rows[:, x * CHUNK_TILES : (x + 1) * CHUNK_TILES, :], in_=z_flipped[:])
-            tiles = slice(h * (HALF // P), (h + 1) * (HALF // P))
+        for c in range(CHUNKS):
+            h, j = divmod(c, HALF_CHUNKS)
+            cols = slice(j * CHUNK, (j + 1) * CHUNK)
+            tiles = slice(c * CHUNK_TILES, (c + 1) * CHUNK_TILES)
+            z_t = tail.tile([P, CHUNK_TILES, P], F32, name="z_t%d" % c)
+            nc.vector.tensor_tensor(out=z_t[:].rearrange("p i q -> p (i q)"), in0=noise[h][:, cols], in1=mean[h][:, cols], op=ALU.add)
+            z_flipped = flip_psum.tile([P, CHUNK_TILES, C], F32, tag="flip")
+            for i in range(CHUNK_TILES):
+                nc.tensor.transpose(z_flipped[:, i, :], z_t[:, i, :], ident_f32[:])
+            nc.scalar.copy(out=z_rows[:, tiles, :], in_=z_flipped[:])
             nc.sync.dma_start(out=out_rows[:, tiles, :], in_=z_rows[:, tiles, :])

@@ -27,14 +27,23 @@ HALF = 512
 HALVES = ROWS // HALF
 HALF_CHUNKS = HALF // CHUNK
 RUN = 4
-AHEAD = HALF_CHUNKS + CHUNKS
 BN_STATS_DIM = 6
 BN_AGGR_DIM = 2
 BN_EPS = 1e-5
 HEADS = 2
+TAIL_PASSES = 9
 MEAN, LOGVAR = 0, 1
 
+EN2_PIECES = ((0, 256), (256, 256), (512, 256), (768, 128), (896, 128))
+Z_PIECES = ((0, 128), (128, 384), (512, 384), (896, 128))
+
 FLOPS = 2 * ROWS * K * K + 2 * 2 * ROWS * K * C
+
+
+def half_of(piece):
+    first, width = piece
+    h = first // HALF
+    return h, slice(first - h * HALF, first - h * HALF + width)
 
 
 def tile_model_pa_kernel(tc, en1, eps, W2, b2, Wm, Wv, gm, betam, gv, betav, out):
@@ -43,7 +52,7 @@ def tile_model_pa_kernel(tc, en1, eps, W2, b2, Wm, Wv, gm, betam, gv, betav, out
         const = ctx.enter_context(tc.tile_pool(name="const", bufs=1))
         raw = ctx.enter_context(tc.tile_pool(name="raw", bufs=1))
         keep = ctx.enter_context(tc.tile_pool(name="keep", bufs=1))
-        stage = ctx.enter_context(tc.tile_pool(name="stage", bufs=3))
+        stage = ctx.enter_context(tc.tile_pool(name="stage", bufs=4))
         tail = ctx.enter_context(tc.tile_pool(name="tail", bufs=1))
         flip_psum = ctx.enter_context(tc.psum_pool(name="flip_psum", bufs=4))
         acc_psum = ctx.enter_context(tc.psum_pool(name="acc_psum", bufs=4))
@@ -70,16 +79,15 @@ def tile_model_pa_kernel(tc, en1, eps, W2, b2, Wm, Wv, gm, betam, gv, betav, out
             g, pair = divmod(c, PACK // CHUNK_TILES)
             return (w2_rows[:, g, pair * CHUNK_TILES : (pair + 1) * CHUNK_TILES, :], w_codes[c][:], w_scales[c][:])
 
-        chunks = [x_chunk(c) for c in range(HALF_CHUNKS)]
-        chunks.extend([w_chunk(c) for c in range(CHUNKS)])
-        chunks.extend([x_chunk(c) for c in range(HALF_CHUNKS, CHUNKS)])
+        order = [("x", 0), ("w", 0), ("x", 1), ("w", 1), ("w", 2), ("w", 3), ("x", 2), ("x", 3)]
+        chunks = {key: (x_chunk if key[0] == "x" else w_chunk)(key[1]) for key in order}
 
         b2_bf = const.tile([P, PASSES, PACK], BF16)
         with nc.allow_non_contiguous_dma(reason="8 bytes of b2 to a partition and pass"):
             nc.scalar.dma_start(out=b2_bf[:], in_=b2_cols)
-        chunk_raw = [raw.tile([P, CHUNK_TILES, K], BF16, name="chunk_raw%d" % n) for n in range(len(chunks))]
-        for n in range(len(chunks)):
-            nc.sync.dma_start(out=chunk_raw[n][:], in_=chunks[n][0])
+        chunk_raw = {key: raw.tile([P, CHUNK_TILES, K], BF16, name="raw_%s%d" % key) for key in order}
+        for key in order:
+            nc.sync.dma_start(out=chunk_raw[key][:], in_=chunks[key][0])
         wm_raw = raw.tile([P, K], BF16)
         wv_raw = raw.tile([P, K], BF16)
         eps_raw = raw.tile([P, ROW_TILES, C], BF16)
@@ -108,12 +116,13 @@ def tile_model_pa_kernel(tc, en1, eps, W2, b2, Wm, Wv, gm, betam, gv, betav, out
         nc.vector.tensor_copy(out=b2_f32[:], in_=b2_bf[:].rearrange("p g t -> p (g t)"))
 
         grouped = {}
+        acc = {}
 
-        def flip(n):
-            grouped[n] = stage.tile([P, PASSES * CHUNK * PACK], BF16, tag="grouped", name="grouped%d" % n, align_bytes=64)
-            grouped_words = grouped[n][:].bitcast(F32).rearrange("p (g r u) -> p g r u", g=PASSES, u=PAIRS)
+        def flip(key, on_scalar=(1,)):
+            grouped[key] = stage.tile([P, PASSES * CHUNK * PACK], BF16, tag="grouped", name="grouped_%s%d" % key, align_bytes=64)
+            grouped_words = grouped[key][:].bitcast(F32).rearrange("p (g r u) -> p g r u", g=PASSES, u=PAIRS)
             for i in range(CHUNK_TILES):
-                words = chunk_raw[n][:, i, :].bitcast(F32)
+                words = chunk_raw[key][:, i, :].bitcast(F32)
                 flipped = flip_psum.tile([P, PASSES, PAIRS, P], F32, tag="flip")
                 for g in range(PASSES):
                     for u in range(PAIRS):
@@ -121,51 +130,70 @@ def tile_model_pa_kernel(tc, en1, eps, W2, b2, Wm, Wv, gm, betam, gv, betav, out
                         nc.tensor.transpose(flipped[:, g, u, :], words[:, block * P : (block + 1) * P], ident_f32[:])
                 dst = grouped_words[:, :, i * P : (i + 1) * P, :]
                 src = flipped[:].rearrange("p g u r -> p g r u")
-                if i % 2 == 0:
-                    nc.vector.tensor_copy(out=dst, in_=src)
-                else:
+                if i in on_scalar:
                     nc.scalar.copy(out=dst, in_=src)
+                else:
+                    nc.vector.tensor_copy(out=dst, in_=src)
 
-        def quantise(n):
-            codes, scales = chunks[n][1], chunks[n][2]
+        def quantise(key):
+            codes, scales = chunks[key][1], chunks[key][2]
             width = CHUNK * PACK
             for g in range(PASSES):
                 nc.vector.quantize_mx(
                     out=codes[:, g, :].bitcast(FP8X4),
                     scales=scales[:, g, :],
-                    in_=grouped[n][:, g * width : (g + 1) * width],
+                    in_=grouped[key][:, g * width : (g + 1) * width],
                 )
 
-        def multiply(c, h):
+        def multiply(c, h, cols=slice(0, HALF)):
             for i in range(CHUNK_TILES):
-                m = c * CHUNK_TILES + i
+                if (c, h, i) not in acc:
+                    acc[c, h, i] = acc_psum.tile([P, HALF], F32, tag="acc", name="acc%d%d%d" % (c, h, i))
                 m_cols = slice(i * P, (i + 1) * P)
-                acc = acc_psum.tile([P, HALF], F32, tag="acc")
                 for g in range(PASSES):
                     nc.tensor.matmul_mx(
-                        out=acc[:],
+                        out=acc[c, h, i][:, cols],
                         lhsT=w_codes[c][:, g, m_cols].bitcast(FP8X4),
                         lhsT_scale=w_scales[c][:, g, m_cols],
-                        rhs=x_codes[h][:, g, :].bitcast(FP8X4),
-                        rhs_scale=x_scales[h][:, g, :],
+                        rhs=x_codes[h][:, g, cols].bitcast(FP8X4),
+                        rhs_scale=x_scales[h][:, g, cols],
                         start=(g == 0),
                         stop=(g == PASSES - 1),
                     )
-                nc.scalar.activation(out=exp_v[h][:, m, :], in_=acc[:], func=ACT.Exp, bias=b2_f32[:, m : m + 1], scale=1.0)
 
-        for n in range(AHEAD):
-            flip(n)
-            if n > 0:
-                quantise(n - 1)
-        for c in range(CHUNKS):
-            multiply(c, 0)
-            n = AHEAD + c
-            if n < len(chunks):
-                flip(n)
-            if n <= len(chunks):
-                quantise(n - 1)
+        def exponentials(c, h):
+            for i in range(CHUNK_TILES):
+                m = c * CHUNK_TILES + i
+                nc.scalar.activation(out=exp_v[h][:, m, :], in_=acc[c, h, i][:], func=ACT.Exp, bias=b2_f32[:, m : m + 1], scale=1.0)
+
+        flip(("x", 0))
+        quantise(("x", 0))
+        flip(("w", 0))
+        quantise(("w", 0))
+        flip(("x", 1), on_scalar=(0, 1))
+        flip(("w", 1))
+        multiply(0, 0, slice(0, CHUNK))
+        quantise(("x", 1))
+        quantise(("w", 1))
+        flip(("w", 2))
+        multiply(0, 0, slice(CHUNK, HALF))
+        exponentials(0, 0)
+        flip(("w", 3))
+        quantise(("w", 2))
+        multiply(1, 0)
+        exponentials(1, 0)
+        flip(("x", 2))
+        flip(("x", 3))
+        quantise(("w", 3))
+        multiply(2, 0)
+        exponentials(2, 0)
+        quantise(("x", 2))
+        quantise(("x", 3))
+        multiply(3, 0)
+        exponentials(3, 0)
         for c in range(CHUNKS):
             multiply(c, 1)
+            exponentials(c, 1)
 
         head_grouped = keep.tile([P, HEADS * PASSES * C * PACK], BF16, align_bytes=64)
         head_words = head_grouped[:].bitcast(F32).rearrange("p (s g c u) -> p s g c u", s=HEADS, g=PASSES, u=PAIRS)
@@ -198,55 +226,73 @@ def tile_model_pa_kernel(tc, en1, eps, W2, b2, Wm, Wv, gm, betam, gv, betav, out
         nc.vector.tensor_scalar(out=beta[:, LOGVAR : LOGVAR + 1], in0=betav_bf[:], scalar1=0.5, scalar2=None, op0=ALU.mult)
 
         hidden = [[acc_psum.tile([P, HALF], F32, tag="acc", name="hidden%d%d" % (s, h)) for h in range(HALVES)] for s in range(HEADS)]
-        stats = keep.tile([P, HEADS, CHUNKS, BN_STATS_DIM], F32)
+        stats = keep.tile([P, HEADS, len(EN2_PIECES), BN_STATS_DIM], F32)
         table_scratch = const.tile([P, 1], F32)
 
-        def statistics(c, s):
-            h, j = divmod(c, HALF_CHUNKS)
-            nc.vector.bn_stats(out=stats[:, s, c, :], in_=hidden[s][h][:, j * CHUNK : (j + 1) * CHUNK])
+        def statistics(n, s):
+            h, cols = half_of(EN2_PIECES[n])
+            nc.vector.bn_stats(out=stats[:, s, n, :], in_=hidden[s][h][:, cols])
 
-        for c in range(CHUNKS):
-            h, j = divmod(c, HALF_CHUNKS)
-            cols = slice(j * CHUNK, (j + 1) * CHUNK)
+        idle = flip_psum.tile([P, HALF], F32, tag="flip")
+
+        def idle_passes(count):
+            for n in range(count):
+                nc.tensor.matmul_mx(
+                    out=idle[:],
+                    lhsT=head_codes[:, MEAN, 0, :].bitcast(FP8X4),
+                    lhsT_scale=head_scales[:, MEAN, 0, :],
+                    rhs=x_codes[0][:, 0, :].bitcast(FP8X4),
+                    rhs_scale=x_scales[0][:, 0, :],
+                    start=True,
+                    stop=True,
+                )
+
+        heads_in_order = (LOGVAR, MEAN)
+        for n in range(len(EN2_PIECES)):
+            h, cols = half_of(EN2_PIECES[n])
+            width = EN2_PIECES[n][1]
             for g in range(PASSES):
                 en2 = stage.tile([P, CHUNK * PACK], BF16, tag="en2", align_bytes=64)
                 en2_codes = stage.tile([P, CHUNK], U32, tag="en2_codes", align_bytes=64)
                 en2_scales = stage.tile([P, CHUNK], U8, tag="en2_scales", align_bytes=64)
                 nc.scalar.activation(
-                    out=en2[:].rearrange("p (a i t) -> p a t i", i=RUN, t=PACK),
+                    out=en2[:, : width * PACK].rearrange("p (a i t) -> p a t i", i=RUN, t=PACK),
                     in_=exp_v[h][:, g * PACK : (g + 1) * PACK, cols].rearrange("p t (a i) -> p a t i", i=RUN),
                     func=ACT.Ln,
                     bias=one[:],
                     scale=1.0,
                 )
-                nc.vector.quantize_mx(out=en2_codes[:].bitcast(FP8X4), scales=en2_scales[:], in_=en2[:])
+                nc.vector.quantize_mx(
+                    out=en2_codes[:, :width].bitcast(FP8X4), scales=en2_scales[:, :width], in_=en2[:, : width * PACK]
+                )
+                if n > 0:
+                    statistics(n - 1, heads_in_order[g])
                 for s in (LOGVAR, MEAN):
                     nc.tensor.matmul_mx(
                         out=hidden[s][h][:, cols],
                         lhsT=head_codes[:, s, g, :].bitcast(FP8X4),
                         lhsT_scale=head_scales[:, s, g, :],
-                        rhs=en2_codes[:].bitcast(FP8X4),
-                        rhs_scale=en2_scales[:],
+                        rhs=en2_codes[:, :width].bitcast(FP8X4),
+                        rhs_scale=en2_scales[:, :width],
                         start=(g == 0),
                         stop=(g == PASSES - 1),
                     )
-            if c > 0:
-                for s in (LOGVAR, MEAN):
-                    statistics(c - 1, s)
+                idle_passes(1)
+            if n == 1:
+                even_spread = stats[:, :, 0, 2:3]
+                nc.vector.tensor_scalar(out=even_spread, in0=even_spread, scalar1=ROWS * BN_EPS, scalar2=None, op0=ALU.add)
         nc.scalar.activation(out=table_scratch[:], in_=en2[:, 0:1], func=ACT.Exp)
 
         rstd = [const.tile([P, 1], F32, name="rstd%d" % s) for s in range(HEADS)]
         mean_var = const.tile([P, HEADS, BN_AGGR_DIM], F32)
-        var_eps = const.tile([P, HEADS], F32)
         neg_mean_gamma = const.tile([P, HEADS], F32)
         gain = const.tile([P, HEADS], F32)
         shift = const.tile([P, HEADS], F32)
         for s in (LOGVAR, MEAN):
             col = slice(s, s + 1)
-            statistics(CHUNKS - 1, s)
+            statistics(len(EN2_PIECES) - 1, s)
             nc.vector.bn_aggr(out=mean_var[:, s, :], in_=stats[:, s, :, :].rearrange("p c k -> p (c k)"))
-            nc.vector.tensor_scalar(out=var_eps[:, col], in0=mean_var[:, s, 1:2], scalar1=BN_EPS, scalar2=None, op0=ALU.add)
-            nc.gpsimd.tensor_tensor(out=rstd[s][:], in0=var_eps[:, col], in1=neg_half[:], op=ALU.pow)
+            nc.gpsimd.tensor_tensor(out=rstd[s][:], in0=mean_var[:, s, 1:2], in1=neg_half[:], op=ALU.pow)
             nc.vector.scalar_tensor_tensor(
                 out=neg_mean_gamma[:, col], in0=mean_var[:, s, 0:1], scalar=-1.0, in1=gamma[:, col], op0=ALU.mult, op1=ALU.mult
             )
@@ -257,31 +303,44 @@ def tile_model_pa_kernel(tc, en1, eps, W2, b2, Wm, Wv, gm, betam, gv, betav, out
                 out=shift[:, col], in0=neg_mean_gamma[:, col], scalar1=rstd[s][:], scalar2=beta[:, col], op0=ALU.mult, op1=ALU.add
             )
 
-        std = [tail.tile([P, HALF], F32, name="std%d" % h) for h in range(HALVES)]
-        mean = [tail.tile([P, HALF], F32, name="mean%d" % h) for h in range(HALVES)]
-        noise = [tail.tile([P, HALF], F32, name="noise%d" % h) for h in range(HALVES)]
-        for h in range(HALVES):
+        idle_passes(TAIL_PASSES)
+
+        z_rows = keep.tile([P, ROW_TILES, C], F32)
+        pieces = range(len(Z_PIECES))
+        std = [tail.tile([P, Z_PIECES[n][1]], F32, name="std%d" % n) for n in pieces]
+        mean = [tail.tile([P, Z_PIECES[n][1]], F32, name="mean%d" % n) for n in pieces]
+        noise = [tail.tile([P, Z_PIECES[n][1]], F32, name="noise%d" % n) for n in pieces]
+        z_t = [tail.tile([P, Z_PIECES[n][1]], F32, name="z_t%d" % n) for n in pieces]
+        z_flipped = [flip_psum.tile([P, Z_PIECES[n][1] // P, C], F32, tag="flip", name="z_flipped%d" % n) for n in pieces]
+
+        def row_tiles(n):
+            first, width = Z_PIECES[n]
+            return slice(first // P, (first + width) // P)
+
+        def noise_of(n):
+            h, cols = half_of(Z_PIECES[n])
             nc.scalar.activation(
-                out=std[h][:], in_=hidden[LOGVAR][h][:], func=ACT.Exp,
+                out=std[n][:], in_=hidden[LOGVAR][h][:, cols], func=ACT.Exp,
                 bias=shift[:, LOGVAR : LOGVAR + 1], scale=gain[:, LOGVAR : LOGVAR + 1],
             )
-        for h in range(HALVES):
+            eps_cols = eps_t[:, row_tiles(n), :].rearrange("p r q -> p (r q)")
+            nc.vector.tensor_tensor(out=noise[n][:], in0=std[n][:], in1=eps_cols, op=ALU.mult)
+
+        def sample(n):
+            h, cols = half_of(Z_PIECES[n])
             nc.scalar.activation(
-                out=mean[h][:], in_=hidden[MEAN][h][:], func=ACT.Identity,
+                out=mean[n][:], in_=hidden[MEAN][h][:, cols], func=ACT.Identity,
                 bias=shift[:, MEAN : MEAN + 1], scale=gain[:, MEAN : MEAN + 1],
             )
-        for h in range(HALVES):
-            tiles = slice(h * (HALF // P), (h + 1) * (HALF // P))
-            nc.vector.tensor_tensor(out=noise[h][:], in0=std[h][:], in1=eps_t[:, tiles, :].rearrange("p r q -> p (r q)"), op=ALU.mult)
-        z_rows = keep.tile([P, ROW_TILES, C], F32)
-        for c in range(CHUNKS):
-            h, j = divmod(c, HALF_CHUNKS)
-            cols = slice(j * CHUNK, (j + 1) * CHUNK)
-            tiles = slice(c * CHUNK_TILES, (c + 1) * CHUNK_TILES)
-            z_t = tail.tile([P, CHUNK_TILES, P], F32, name="z_t%d" % c)
-            nc.vector.tensor_tensor(out=z_t[:].rearrange("p i q -> p (i q)"), in0=noise[h][:, cols], in1=mean[h][:, cols], op=ALU.add)
-            z_flipped = flip_psum.tile([P, CHUNK_TILES, C], F32, tag="flip")
-            for i in range(CHUNK_TILES):
-                nc.tensor.transpose(z_flipped[:, i, :], z_t[:, i, :], ident_f32[:])
-            nc.scalar.copy(out=z_rows[:, tiles, :], in_=z_flipped[:])
-            nc.sync.dma_start(out=out_rows[:, tiles, :], in_=z_rows[:, tiles, :])
+            nc.vector.tensor_tensor(out=z_t[n][:], in0=noise[n][:], in1=mean[n][:], op=ALU.add)
+            for i in range(Z_PIECES[n][1] // P):
+                nc.tensor.transpose(z_flipped[n][:, i, :], z_t[n][:, i * P : (i + 1) * P], ident_f32[:])
+
+        noise_of(0)
+        for n in pieces[1:]:
+            noise_of(n)
+            sample(n - 1)
+        sample(len(Z_PIECES) - 1)
+        for n in pieces:
+            nc.scalar.copy(out=z_rows[:, row_tiles(n), :], in_=z_flipped[n][:])
+            nc.sync.dma_start(out=out_rows[:, row_tiles(n), :], in_=z_rows[:, row_tiles(n), :])

@@ -31,6 +31,7 @@ BN_STATS_DIM = 6
 BN_AGGR_DIM = 2
 BN_EPS = 1e-5
 HEADS = 2
+HEAD_MATMULS = 5
 TAIL_PASSES = 9
 MEAN, LOGVAR = 0, 1
 
@@ -104,6 +105,8 @@ def tile_model_pa_kernel(tc, en1, eps, W2, b2, Wm, Wv, gm, betam, gv, betav, out
             nc.sync.dma_start(out=betam_bf[:], in_=betam.rearrange("(p o) -> p o", o=1))
             nc.sync.dma_start(out=betav_bf[:], in_=betav.rearrange("(p o) -> p o", o=1))
 
+        zeros = const.tile([P, HALF], BF16)
+        nc.vector.memset(zeros[:], 0.0)
         ident_f32 = const.tile([P, P], F32)
         masks.make_identity(nc, ident_f32[:])
         ident_bf = const.tile([P, P], BF16)
@@ -166,11 +169,21 @@ def tile_model_pa_kernel(tc, en1, eps, W2, b2, Wm, Wv, gm, betam, gv, betav, out
                 m = c * CHUNK_TILES + i
                 nc.scalar.activation(out=exp_v[h][:, m, :], in_=acc[c, h, i][:], func=ACT.Exp, bias=b2_f32[:, m : m + 1], scale=1.0)
 
+        head_idle = acc_psum.tile([P, HALF], F32, tag="acc", name="head_idle")
+
+        def idle_matmuls(count):
+            for n in range(count):
+                nc.tensor.matmul(head_idle[:], lhsT=zeros[:, :P], rhs=zeros[:], start=True, stop=True)
+
+        idle_matmuls(HEAD_MATMULS)
         flip(("x", 0))
+        idle_matmuls(1)
         quantise(("x", 0))
         flip(("w", 0))
+        idle_matmuls(1)
         quantise(("w", 0))
         flip(("x", 1), on_scalar=(0, 1))
+        idle_matmuls(1)
         flip(("w", 1))
         multiply(0, 0, slice(0, CHUNK))
         quantise(("x", 1))

@@ -31,7 +31,7 @@ BN_STATS_DIM = 6
 BN_AGGR_DIM = 2
 BN_EPS = 1e-5
 HEADS = 2
-HEAD_MATMULS = 5
+HEAD_MATMULS = 8
 TAIL_PASSES = 9
 MEAN, LOGVAR = 0, 1
 
@@ -69,7 +69,7 @@ def tile_model_pa_kernel(tc, en1, eps, W2, b2, Wm, Wv, gm, betam, gv, betav, out
         x_scales = [keep.tile([P, PASSES, HALF], U8, name="x_scales%d" % h, align_bytes=64) for h in range(HALVES)]
         w_codes = [keep.tile([P, PASSES, CHUNK], U32, name="w_codes%d" % c, align_bytes=64) for c in range(CHUNKS)]
         w_scales = [keep.tile([P, PASSES, CHUNK], U8, name="w_scales%d" % c, align_bytes=64) for c in range(CHUNKS)]
-        exp_v = [keep.tile([P, PASSES * PACK, HALF], F32, name="exp_v%d" % h) for h in range(HALVES)]
+        exp_v = [keep.tile([P, PASSES, HALF // RUN, PACK, RUN], F32, name="exp_v%d" % h) for h in range(HALVES)]
 
         def x_chunk(c):
             h, j = divmod(c, HALF_CHUNKS)
@@ -105,7 +105,7 @@ def tile_model_pa_kernel(tc, en1, eps, W2, b2, Wm, Wv, gm, betam, gv, betav, out
             nc.sync.dma_start(out=betam_bf[:], in_=betam.rearrange("(p o) -> p o", o=1))
             nc.sync.dma_start(out=betav_bf[:], in_=betav.rearrange("(p o) -> p o", o=1))
 
-        zeros = const.tile([P, HALF], BF16)
+        zeros = const.tile([P, CHUNK], BF16)
         nc.vector.memset(zeros[:], 0.0)
         ident_f32 = const.tile([P, P], F32)
         masks.make_identity(nc, ident_f32[:])
@@ -167,23 +167,30 @@ def tile_model_pa_kernel(tc, en1, eps, W2, b2, Wm, Wv, gm, betam, gv, betav, out
         def exponentials(c, h):
             for i in range(CHUNK_TILES):
                 m = c * CHUNK_TILES + i
-                nc.scalar.activation(out=exp_v[h][:, m, :], in_=acc[c, h, i][:], func=ACT.Exp, bias=b2_f32[:, m : m + 1], scale=1.0)
+                g, t = divmod(m, PACK)
+                nc.scalar.activation(
+                    out=exp_v[h][:, g, :, t, :],
+                    in_=acc[c, h, i][:].rearrange("p (a i) -> p a i", i=RUN),
+                    func=ACT.Exp,
+                    bias=b2_f32[:, m : m + 1],
+                    scale=1.0,
+                )
 
         head_idle = acc_psum.tile([P, HALF], F32, tag="acc", name="head_idle")
 
         def idle_matmuls(count):
             for n in range(count):
-                nc.tensor.matmul(head_idle[:], lhsT=zeros[:, :P], rhs=zeros[:], start=True, stop=True)
+                nc.tensor.matmul(head_idle[:, :CHUNK], lhsT=zeros[:, :P], rhs=zeros[:], start=True, stop=True)
 
         idle_matmuls(HEAD_MATMULS)
         flip(("x", 0))
-        idle_matmuls(1)
+        idle_matmuls(2)
         quantise(("x", 0))
         flip(("w", 0))
-        idle_matmuls(1)
+        idle_matmuls(2)
         quantise(("w", 0))
         flip(("x", 1), on_scalar=(0, 1))
-        idle_matmuls(1)
+        idle_matmuls(2)
         flip(("w", 1))
         multiply(0, 0, slice(0, CHUNK))
         quantise(("x", 1))
@@ -270,7 +277,7 @@ def tile_model_pa_kernel(tc, en1, eps, W2, b2, Wm, Wv, gm, betam, gv, betav, out
                 en2_scales = stage.tile([P, CHUNK], U8, tag="en2_scales", align_bytes=64)
                 nc.scalar.activation(
                     out=en2[:, : width * PACK].rearrange("p (a i t) -> p a t i", i=RUN, t=PACK),
-                    in_=exp_v[h][:, g * PACK : (g + 1) * PACK, cols].rearrange("p t (a i) -> p a t i", i=RUN),
+                    in_=exp_v[h][:, g, cols.start // RUN : cols.stop // RUN, :, :],
                     func=ACT.Ln,
                     bias=one[:],
                     scale=1.0,

@@ -32,10 +32,10 @@ BN_AGGR_DIM = 2
 BN_EPS = 1e-5
 HEADS = 2
 HEAD_MATMULS = 8
-TAIL_PASSES = 9
+TAIL_PASSES = 5
 MEAN, LOGVAR = 0, 1
 
-EN2_PIECES = ((0, 256), (256, 256), (512, 256), (768, 128), (896, 128))
+EN2_PIECES = ((0, 256), (256, 256), (512, 256), (768, 256))
 Z_PIECES = ((0, 128), (128, 384), (512, 384), (896, 128))
 
 FLOPS = 2 * ROWS * K * K + 2 * 2 * ROWS * K * C
@@ -109,8 +109,6 @@ def tile_model_pa_kernel(tc, en1, eps, W2, b2, Wm, Wv, gm, betam, gv, betav, out
         nc.vector.memset(zeros[:], 0.0)
         ident_f32 = const.tile([P, P], F32)
         masks.make_identity(nc, ident_f32[:])
-        ident_bf = const.tile([P, P], BF16)
-        masks.make_identity(nc, ident_bf[:])
         one = const.tile([P, 1], F32)
         nc.vector.memset(one[:], 1.0)
         neg_half = const.tile([P, 1], F32)
@@ -227,11 +225,6 @@ def tile_model_pa_kernel(tc, en1, eps, W2, b2, Wm, Wv, gm, betam, gv, betav, out
                     first = g * PAIRS * P + u
                     nc.tensor.transpose(flipped[:, g, u, :], words[:, first : (g + 1) * PAIRS * P : PAIRS], ident_f32[:])
             nc.vector.tensor_copy(out=head_words[:, s, :, :, :], in_=flipped[:].rearrange("p g u c -> p g c u"))
-        eps_flipped = flip_psum.tile([P, ROW_TILES, P], BF16, tag="flip")
-        for r in range(ROW_TILES):
-            nc.tensor.transpose(eps_flipped[:, r, :], eps_raw[:, r, :], ident_bf[:])
-        eps_t = keep.tile([P, ROW_TILES, P], BF16)
-        nc.vector.tensor_copy(out=eps_t[:], in_=eps_flipped[:])
         nc.vector.quantize_mx(
             out=head_codes[:].rearrange("p s g c -> p (s g c)").bitcast(FP8X4),
             scales=head_scales[:].rearrange("p s g c -> p (s g c)"),
@@ -267,7 +260,6 @@ def tile_model_pa_kernel(tc, en1, eps, W2, b2, Wm, Wv, gm, betam, gv, betav, out
                     stop=True,
                 )
 
-        heads_in_order = (LOGVAR, MEAN)
         for n in range(len(EN2_PIECES)):
             h, cols = half_of(EN2_PIECES[n])
             width = EN2_PIECES[n][1]
@@ -282,11 +274,13 @@ def tile_model_pa_kernel(tc, en1, eps, W2, b2, Wm, Wv, gm, betam, gv, betav, out
                     bias=one[:],
                     scale=1.0,
                 )
+                if n > 0 and g == 0:
+                    statistics(n - 1, LOGVAR)
                 nc.vector.quantize_mx(
                     out=en2_codes[:, :width].bitcast(FP8X4), scales=en2_scales[:, :width], in_=en2[:, : width * PACK]
                 )
-                if n > 0:
-                    statistics(n - 1, heads_in_order[g])
+                if n > 0 and g == 0:
+                    statistics(n - 1, MEAN)
                 for s in (LOGVAR, MEAN):
                     nc.tensor.matmul_mx(
                         out=hidden[s][h][:, cols],
@@ -325,42 +319,37 @@ def tile_model_pa_kernel(tc, en1, eps, W2, b2, Wm, Wv, gm, betam, gv, betav, out
 
         idle_passes(TAIL_PASSES)
 
-        z_rows = keep.tile([P, ROW_TILES, C], F32)
         pieces = range(len(Z_PIECES))
         std = [tail.tile([P, Z_PIECES[n][1]], F32, name="std%d" % n) for n in pieces]
         mean = [tail.tile([P, Z_PIECES[n][1]], F32, name="mean%d" % n) for n in pieces]
-        noise = [tail.tile([P, Z_PIECES[n][1]], F32, name="noise%d" % n) for n in pieces]
-        z_t = [tail.tile([P, Z_PIECES[n][1]], F32, name="z_t%d" % n) for n in pieces]
-        z_flipped = [flip_psum.tile([P, Z_PIECES[n][1] // P, C], F32, tag="flip", name="z_flipped%d" % n) for n in pieces]
+        noise = keep.tile([P, ROW_TILES, C], F32)
+        z_rows = keep.tile([P, ROW_TILES, C], F32)
 
-        def row_tiles(n):
+        def affine_flipped(n, s, func, columns):
+            h, cols = half_of(Z_PIECES[n])
+            col = slice(s, s + 1)
+            nc.scalar.activation(out=columns[:], in_=hidden[s][h][:, cols], func=func, bias=shift[:, col], scale=gain[:, col])
+            row_tiles = Z_PIECES[n][1] // P
+            rows = flip_psum.tile([P, row_tiles, C], F32, tag="flip", name="rows%d%d" % (s, n))
+            for i in range(row_tiles):
+                nc.tensor.transpose(rows[:, i, :], columns[:, i * P : (i + 1) * P], ident_f32[:])
+            return rows
+
+        def tiles_of(n):
             first, width = Z_PIECES[n]
             return slice(first // P, (first + width) // P)
 
-        def noise_of(n):
-            h, cols = half_of(Z_PIECES[n])
-            nc.scalar.activation(
-                out=std[n][:], in_=hidden[LOGVAR][h][:, cols], func=ACT.Exp,
-                bias=shift[:, LOGVAR : LOGVAR + 1], scale=gain[:, LOGVAR : LOGVAR + 1],
-            )
-            eps_cols = eps_t[:, row_tiles(n), :].rearrange("p r q -> p (r q)")
-            nc.vector.tensor_tensor(out=noise[n][:], in0=std[n][:], in1=eps_cols, op=ALU.mult)
+        def make_noise(n):
+            std_rows = affine_flipped(n, LOGVAR, ACT.Exp, std[n])
+            nc.vector.tensor_tensor(out=noise[:, tiles_of(n), :], in0=std_rows[:], in1=eps_raw[:, tiles_of(n), :], op=ALU.mult)
 
-        def sample(n):
-            h, cols = half_of(Z_PIECES[n])
-            nc.scalar.activation(
-                out=mean[n][:], in_=hidden[MEAN][h][:, cols], func=ACT.Identity,
-                bias=shift[:, MEAN : MEAN + 1], scale=gain[:, MEAN : MEAN + 1],
-            )
-            nc.vector.tensor_tensor(out=z_t[n][:], in0=noise[n][:], in1=mean[n][:], op=ALU.add)
-            for i in range(Z_PIECES[n][1] // P):
-                nc.tensor.transpose(z_flipped[n][:, i, :], z_t[n][:, i * P : (i + 1) * P], ident_f32[:])
+        def make_sample(n):
+            mean_rows = affine_flipped(n, MEAN, ACT.Identity, mean[n])
+            nc.vector.tensor_tensor(out=z_rows[:, tiles_of(n), :], in0=mean_rows[:], in1=noise[:, tiles_of(n), :], op=ALU.add)
+            nc.sync.dma_start(out=out_rows[:, tiles_of(n), :], in_=z_rows[:, tiles_of(n), :])
 
-        noise_of(0)
+        make_noise(0)
         for n in pieces[1:]:
-            noise_of(n)
-            sample(n - 1)
-        sample(len(Z_PIECES) - 1)
-        for n in pieces:
-            nc.scalar.copy(out=z_rows[:, row_tiles(n), :], in_=z_flipped[n][:])
-            nc.sync.dma_start(out=out_rows[:, row_tiles(n), :], in_=z_rows[:, row_tiles(n), :])
+            make_noise(n)
+            make_sample(n - 1)
+        make_sample(len(Z_PIECES) - 1)

@@ -26,12 +26,13 @@ CHUNKS = ROWS // CHUNK
 HALF = 512
 HALVES = ROWS // HALF
 HALF_CHUNKS = HALF // CHUNK
-RUN = 4
+RUN = 2
 BN_STATS_DIM = 6
 BN_AGGR_DIM = 2
 BN_EPS = 1e-5
+SPLIT_LOADS = (("x", 0), ("w", 0))
 HEADS = 2
-HEAD_MATMULS = 8
+HEAD_MATMULS = 7
 TAIL_PASSES = 5
 MEAN, LOGVAR = 0, 1
 
@@ -69,7 +70,7 @@ def tile_model_pa_kernel(tc, en1, eps, W2, b2, Wm, Wv, gm, betam, gv, betav, out
         x_scales = [keep.tile([P, PASSES, HALF], U8, name="x_scales%d" % h, align_bytes=64) for h in range(HALVES)]
         w_codes = [keep.tile([P, PASSES, CHUNK], U32, name="w_codes%d" % c, align_bytes=64) for c in range(CHUNKS)]
         w_scales = [keep.tile([P, PASSES, CHUNK], U8, name="w_scales%d" % c, align_bytes=64) for c in range(CHUNKS)]
-        exp_v = [keep.tile([P, PASSES, HALF // RUN, PACK, RUN], F32, name="exp_v%d" % h) for h in range(HALVES)]
+        exp_v = [keep.tile([P, PASSES * PACK, HALF], F32, name="exp_v%d" % h) for h in range(HALVES)]
 
         def x_chunk(c):
             h, j = divmod(c, HALF_CHUNKS)
@@ -88,7 +89,11 @@ def tile_model_pa_kernel(tc, en1, eps, W2, b2, Wm, Wv, gm, betam, gv, betav, out
             nc.scalar.dma_start(out=b2_bf[:], in_=b2_cols)
         chunk_raw = {key: raw.tile([P, CHUNK_TILES, K], BF16, name="raw_%s%d" % key) for key in order}
         for key in order:
-            nc.sync.dma_start(out=chunk_raw[key][:], in_=chunks[key][0])
+            if key in SPLIT_LOADS:
+                for i in range(CHUNK_TILES):
+                    nc.sync.dma_start(out=chunk_raw[key][:, i, :], in_=chunks[key][0][:, i, :])
+            else:
+                nc.sync.dma_start(out=chunk_raw[key][:], in_=chunks[key][0])
         wm_raw = raw.tile([P, K], BF16)
         wv_raw = raw.tile([P, K], BF16)
         eps_raw = raw.tile([P, ROW_TILES, C], BF16)
@@ -119,35 +124,39 @@ def tile_model_pa_kernel(tc, en1, eps, W2, b2, Wm, Wv, gm, betam, gv, betav, out
         grouped = {}
         acc = {}
 
-        def flip(key, on_scalar=(1,)):
-            grouped[key] = stage.tile([P, PASSES * CHUNK * PACK], BF16, tag="grouped", name="grouped_%s%d" % key, align_bytes=64)
-            grouped_words = grouped[key][:].bitcast(F32).rearrange("p (g r u) -> p g r u", g=PASSES, u=PAIRS)
-            for i in range(CHUNK_TILES):
+        def flip(key, tiles=range(CHUNK_TILES), on_scalar=(1,)):
+            whole = len(tiles) == CHUNK_TILES
+            if whole:
+                grouped[key] = stage.tile([P, PASSES * CHUNK * PACK], BF16, tag="grouped", name="grouped_%s%d" % key, align_bytes=64)
+            for i in tiles:
+                if not whole:
+                    grouped[key, i] = stage.tile([P, PASSES * P * PACK], BF16, tag="grouped_tile", name="grouped_%s%d_%d" % (key + (i,)), align_bytes=64)
+                grouped_words = (grouped[key] if whole else grouped[key, i])[:].bitcast(F32).rearrange("p (g r u) -> p g r u", g=PASSES, u=PAIRS)
                 words = chunk_raw[key][:, i, :].bitcast(F32)
                 flipped = flip_psum.tile([P, PASSES, PAIRS, P], F32, tag="flip")
                 for g in range(PASSES):
                     for u in range(PAIRS):
                         block = g * PAIRS + u
                         nc.tensor.transpose(flipped[:, g, u, :], words[:, block * P : (block + 1) * P], ident_f32[:])
-                dst = grouped_words[:, :, i * P : (i + 1) * P, :]
+                dst = grouped_words[:, :, i * P : (i + 1) * P, :] if whole else grouped_words
                 src = flipped[:].rearrange("p g u r -> p g r u")
                 if i in on_scalar:
                     nc.scalar.copy(out=dst, in_=src)
                 else:
                     nc.vector.tensor_copy(out=dst, in_=src)
 
-        def quantise(key):
+        def quantise(key, tile=None):
             codes, scales = chunks[key][1], chunks[key][2]
-            width = CHUNK * PACK
+            cols = slice(0, CHUNK) if tile is None else slice(tile * P, (tile + 1) * P)
+            source = grouped[key] if tile is None else grouped[key, tile]
+            width = (cols.stop - cols.start) * PACK
             for g in range(PASSES):
                 nc.vector.quantize_mx(
-                    out=codes[:, g, :].bitcast(FP8X4),
-                    scales=scales[:, g, :],
-                    in_=grouped[key][:, g * width : (g + 1) * width],
+                    out=codes[:, g, cols].bitcast(FP8X4), scales=scales[:, g, cols], in_=source[:, g * width : (g + 1) * width]
                 )
 
-        def multiply(c, h, cols=slice(0, HALF)):
-            for i in range(CHUNK_TILES):
+        def multiply(c, h, cols=slice(0, HALF), tiles=range(CHUNK_TILES)):
+            for i in tiles:
                 if (c, h, i) not in acc:
                     acc[c, h, i] = acc_psum.tile([P, HALF], F32, tag="acc", name="acc%d%d%d" % (c, h, i))
                 m_cols = slice(i * P, (i + 1) * P)
@@ -165,14 +174,7 @@ def tile_model_pa_kernel(tc, en1, eps, W2, b2, Wm, Wv, gm, betam, gv, betav, out
         def exponentials(c, h):
             for i in range(CHUNK_TILES):
                 m = c * CHUNK_TILES + i
-                g, t = divmod(m, PACK)
-                nc.scalar.activation(
-                    out=exp_v[h][:, g, :, t, :],
-                    in_=acc[c, h, i][:].rearrange("p (a i) -> p a i", i=RUN),
-                    func=ACT.Exp,
-                    bias=b2_f32[:, m : m + 1],
-                    scale=1.0,
-                )
+                nc.scalar.activation(out=exp_v[h][:, m, :], in_=acc[c, h, i][:], func=ACT.Exp, bias=b2_f32[:, m : m + 1], scale=1.0)
 
         head_idle = acc_psum.tile([P, HALF], F32, tag="acc", name="head_idle")
 
@@ -181,17 +183,22 @@ def tile_model_pa_kernel(tc, en1, eps, W2, b2, Wm, Wv, gm, betam, gv, betav, out
                 nc.tensor.matmul(head_idle[:, :CHUNK], lhsT=zeros[:, :P], rhs=zeros[:], start=True, stop=True)
 
         idle_matmuls(HEAD_MATMULS)
-        flip(("x", 0))
+        flip(("x", 0), (0,))
+        quantise(("x", 0), 0)
+        flip(("x", 0), (1,))
         idle_matmuls(2)
-        quantise(("x", 0))
-        flip(("w", 0))
+        flip(("w", 0), (0,))
+        quantise(("x", 0), 1)
+        quantise(("w", 0), 0)
+        flip(("w", 0), (1,))
         idle_matmuls(2)
-        quantise(("w", 0))
-        flip(("x", 1), on_scalar=(0, 1))
-        idle_matmuls(2)
-        flip(("w", 1))
+        quantise(("w", 0), 1)
+        flip(("x", 1), (0,), on_scalar=(0,))
+        flip(("x", 1), (1,), on_scalar=())
         multiply(0, 0, slice(0, CHUNK))
-        quantise(("x", 1))
+        quantise(("x", 1), 0)
+        quantise(("x", 1), 1)
+        flip(("w", 1))
         quantise(("w", 1))
         flip(("w", 2))
         multiply(0, 0, slice(CHUNK, HALF))
@@ -269,7 +276,7 @@ def tile_model_pa_kernel(tc, en1, eps, W2, b2, Wm, Wv, gm, betam, gv, betav, out
                 en2_scales = stage.tile([P, CHUNK], U8, tag="en2_scales", align_bytes=64)
                 nc.scalar.activation(
                     out=en2[:, : width * PACK].rearrange("p (a i t) -> p a t i", i=RUN, t=PACK),
-                    in_=exp_v[h][:, g, cols.start // RUN : cols.stop // RUN, :, :],
+                    in_=exp_v[h][:, g * PACK : (g + 1) * PACK, cols].rearrange("p t (a i) -> p a t i", i=RUN),
                     func=ACT.Ln,
                     bias=one[:],
                     scale=1.0,

@@ -85,8 +85,6 @@ def tile_model_pa_kernel(tc, en1, eps, W2, b2, Wm, Wv, gm, betam, gv, betav, out
         chunks = {key: (x_chunk if key[0] == "x" else w_chunk)(key[1]) for key in order}
 
         b2_bf = const.tile([P, PASSES, PACK], BF16)
-        with nc.allow_non_contiguous_dma(reason="8 bytes of b2 to a partition and pass"):
-            nc.scalar.dma_start(out=b2_bf[:], in_=b2_cols)
         chunk_raw = {key: raw.tile([P, CHUNK_TILES, K], BF16, name="raw_%s%d" % key) for key in order}
         for key in order:
             if key in SPLIT_LOADS:
@@ -94,6 +92,9 @@ def tile_model_pa_kernel(tc, en1, eps, W2, b2, Wm, Wv, gm, betam, gv, betav, out
                     nc.sync.dma_start(out=chunk_raw[key][:, i, :], in_=chunks[key][0][:, i, :])
             else:
                 nc.sync.dma_start(out=chunk_raw[key][:], in_=chunks[key][0])
+            if key == ("x", 1):
+                with nc.allow_non_contiguous_dma(reason="8 bytes of b2 to a partition and pass"):
+                    nc.sync.dma_start(out=b2_bf[:], in_=b2_cols)
         wm_raw = raw.tile([P, K], BF16)
         wv_raw = raw.tile([P, K], BF16)
         eps_raw = raw.tile([P, ROW_TILES, C], BF16)
@@ -118,8 +119,6 @@ def tile_model_pa_kernel(tc, en1, eps, W2, b2, Wm, Wv, gm, betam, gv, betav, out
         nc.vector.memset(one[:], 1.0)
         neg_half = const.tile([P, 1], F32)
         nc.vector.memset(neg_half[:], -0.5)
-        b2_f32 = const.tile([P, PASSES * PACK], F32)
-        nc.vector.tensor_copy(out=b2_f32[:], in_=b2_bf[:].rearrange("p g t -> p (g t)"))
 
         grouped = {}
         acc = {}
@@ -149,6 +148,11 @@ def tile_model_pa_kernel(tc, en1, eps, W2, b2, Wm, Wv, gm, betam, gv, betav, out
             codes, scales = chunks[key][1], chunks[key][2]
             cols = slice(0, CHUNK) if tile is None else slice(tile * P, (tile + 1) * P)
             source = grouped[key] if tile is None else grouped[key, tile]
+            if key[0] == "w" and tile is None:
+                nc.vector.quantize_mx(
+                    out=codes.rearrange("p g m -> p (g m)").bitcast(FP8X4), scales=scales.rearrange("p g m -> p (g m)"), in_=source[:]
+                )
+                return
             width = (cols.stop - cols.start) * PACK
             for g in range(PASSES):
                 nc.vector.quantize_mx(
@@ -171,10 +175,11 @@ def tile_model_pa_kernel(tc, en1, eps, W2, b2, Wm, Wv, gm, betam, gv, betav, out
                         stop=(g == PASSES - 1),
                     )
 
-        def exponentials(c, h):
+        def exponentials(c, h, cols=slice(0, HALF)):
             for i in range(CHUNK_TILES):
                 m = c * CHUNK_TILES + i
-                nc.scalar.activation(out=exp_v[h][:, m, :], in_=acc[c, h, i][:], func=ACT.Exp, bias=b2_f32[:, m : m + 1], scale=1.0)
+                g, t = divmod(m, PACK)
+                nc.scalar.activation(out=exp_v[h][:, m, cols], in_=acc[c, h, i][:, cols], func=ACT.Exp, bias=b2_bf[:, g, t : t + 1], scale=1.0)
 
         head_idle = acc_psum.tile([P, HALF], F32, tag="acc", name="head_idle")
 
@@ -196,13 +201,14 @@ def tile_model_pa_kernel(tc, en1, eps, W2, b2, Wm, Wv, gm, betam, gv, betav, out
         flip(("x", 1), (0,), on_scalar=(0,))
         flip(("x", 1), (1,), on_scalar=())
         multiply(0, 0, slice(0, CHUNK))
+        exponentials(0, 0, slice(0, CHUNK))
         quantise(("x", 1), 0)
         quantise(("x", 1), 1)
         flip(("w", 1))
         quantise(("w", 1))
         flip(("w", 2))
         multiply(0, 0, slice(CHUNK, HALF))
-        exponentials(0, 0)
+        exponentials(0, 0, slice(CHUNK, HALF))
         flip(("w", 3))
         quantise(("w", 2))
         multiply(1, 0)
@@ -274,18 +280,22 @@ def tile_model_pa_kernel(tc, en1, eps, W2, b2, Wm, Wv, gm, betam, gv, betav, out
                 en2 = stage.tile([P, CHUNK * PACK], BF16, tag="en2", align_bytes=64)
                 en2_codes = stage.tile([P, CHUNK], U32, tag="en2_codes", align_bytes=64)
                 en2_scales = stage.tile([P, CHUNK], U8, tag="en2_scales", align_bytes=64)
-                nc.scalar.activation(
-                    out=en2[:, : width * PACK].rearrange("p (a i t) -> p a t i", i=RUN, t=PACK),
-                    in_=exp_v[h][:, g * PACK : (g + 1) * PACK, cols].rearrange("p t (a i) -> p a t i", i=RUN),
-                    func=ACT.Ln,
-                    bias=one[:],
-                    scale=1.0,
-                )
-                if n > 0 and g == 0:
-                    statistics(n - 1, LOGVAR)
-                nc.vector.quantize_mx(
-                    out=en2_codes[:, :width].bitcast(FP8X4), scales=en2_scales[:, :width], in_=en2[:, : width * PACK]
-                )
+                last = n == len(EN2_PIECES) - 1 and g == PASSES - 1
+                step = width // 2 if last else width
+                for first in range(0, width, step):
+                    part = slice(first, first + step)
+                    part_values = en2[:, first * PACK : (first + step) * PACK]
+                    part_cols = slice(cols.start + first, cols.start + first + step)
+                    nc.scalar.activation(
+                        out=part_values.rearrange("p (a i t) -> p a t i", i=RUN, t=PACK),
+                        in_=exp_v[h][:, g * PACK : (g + 1) * PACK, part_cols].rearrange("p t (a i) -> p a t i", i=RUN),
+                        func=ACT.Ln,
+                        bias=one[:],
+                        scale=1.0,
+                    )
+                    if n > 0 and g == 0:
+                        statistics(n - 1, LOGVAR)
+                    nc.vector.quantize_mx(out=en2_codes[:, part].bitcast(FP8X4), scales=en2_scales[:, part], in_=part_values)
                 if n > 0 and g == 0:
                     statistics(n - 1, MEAN)
                 for s in (LOGVAR, MEAN):
@@ -298,7 +308,6 @@ def tile_model_pa_kernel(tc, en1, eps, W2, b2, Wm, Wv, gm, betam, gv, betav, out
                         start=(g == 0),
                         stop=(g == PASSES - 1),
                     )
-                idle_passes(1)
             if n == 1:
                 even_spread = stats[:, :, 0, 2:3]
                 nc.vector.tensor_scalar(out=even_spread, in0=even_spread, scalar1=ROWS * BN_EPS, scalar2=None, op0=ALU.add)

from contextlib import ExitStack

import concourse.masks as masks
import concourse.mybir as mybir

BF16 = mybir.dt.bfloat16
F32 = mybir.dt.float32
U32 = mybir.dt.uint32
U8 = mybir.dt.uint8
FP8X4 = mybir.dt.float8_e4m3fn_x4
ACT = mybir.ActivationFunctionType
ALU = mybir.AluOpType

P = 128
PACK = 4
PAIRS = PACK // 2
K_PASS = P * PACK
ROWS = 1024
K = 1024
C = 128
PASSES = K // K_PASS
ROW_TILES = ROWS // P
CHUNK_TILES = 2
CHUNK = CHUNK_TILES * P
CHUNKS = ROWS // CHUNK
HALF = 512
HALVES = ROWS // HALF
HALF_CHUNKS = HALF // CHUNK
RUN = 2
BN_STATS_DIM = 6
BN_AGGR_DIM = 2
BN_EPS = 1e-5
SPLIT_LOADS = (("x", 0), ("w", 0))
HEADS = 2
HEAD_MATMULS = 7
TAIL_PASSES = 5
MEAN, LOGVAR = 0, 1

EN2_PIECES = ((0, 256), (256, 256), (512, 256), (768, 256))
Z_PIECES = ((0, 128), (128, 384), (512, 384), (896, 128))

FLOPS = 2 * ROWS * K * K + 2 * 2 * ROWS * K * C


def half_of(piece):
    first, width = piece
    h = first // HALF
    return h, slice(first - h * HALF, first - h * HALF + width)


def tile_model_pa_kernel(tc, en1, eps, W2, b2, Wm, Wv, gm, betam, gv, betav, out):
    nc = tc.nc
    with ExitStack() as ctx:
        const = ctx.enter_context(tc.tile_pool(name="const", bufs=1))
        raw = ctx.enter_context(tc.tile_pool(name="raw", bufs=1))
        keep = ctx.enter_context(tc.tile_pool(name="keep", bufs=1))
        stage = ctx.enter_context(tc.tile_pool(name="stage", bufs=4))
        tail = ctx.enter_context(tc.tile_pool(name="tail", bufs=1))
        flip_psum = ctx.enter_context(tc.psum_pool(name="flip_psum", bufs=4))
        acc_psum = ctx.enter_context(tc.psum_pool(name="acc_psum", bufs=4))
        ctx.enter_context(tc.manual_schedule())

        en1_rows = en1.rearrange("(p r) k -> p r k", r=ROW_TILES)
        eps_rows = eps.rearrange("(p r) c -> p r c", r=ROW_TILES)
        out_rows = out.rearrange("(p r) c -> p r c", r=ROW_TILES)
        w2_rows = W2.rearrange("(g p t) k -> p g t k", p=P, t=PACK)
        b2_cols = b2.rearrange("(g p t) -> p g t", p=P, t=PACK)

        x_codes = [keep.tile([P, PASSES, HALF], U32, name="x_codes%d" % h, align_bytes=64) for h in range(HALVES)]
        x_scales = [keep.tile([P, PASSES, HALF], U8, name="x_scales%d" % h, align_bytes=64) for h in range(HALVES)]
        w_codes = [keep.tile([P, PASSES, CHUNK], U32, name="w_codes%d" % c, align_bytes=64) for c in range(CHUNKS)]
        w_scales = [keep.tile([P, PASSES, CHUNK], U8, name="w_scales%d" % c, align_bytes=64) for c in range(CHUNKS)]
        exp_v = [keep.tile([P, PASSES * PACK, HALF], F32, name="exp_v%d" % h) for h in range(HALVES)]

        def x_chunk(c):
            h, j = divmod(c, HALF_CHUNKS)
            cols = slice(j * CHUNK, (j + 1) * CHUNK)
            return (en1_rows[:, c * CHUNK_TILES : (c + 1) * CHUNK_TILES, :], x_codes[h][:, :, cols], x_scales[h][:, :, cols])

        def w_chunk(c):
            g, pair = divmod(c, PACK // CHUNK_TILES)
            return (w2_rows[:, g, pair * CHUNK_TILES : (pair + 1) * CHUNK_TILES, :], w_codes[c][:], w_scales[c][:])

        order = [("x", 0), ("w", 0), ("x", 1), ("w", 1), ("w", 2), ("w", 3), ("x", 2), ("x", 3)]
        chunks = {key: (x_chunk if key[0] == "x" else w_chunk)(key[1]) for key in order}

        b2_bf = const.tile([P, PASSES, PACK], BF16)
        chunk_raw = {key: raw.tile([P, CHUNK_TILES, K], BF16, name="raw_%s%d" % key) for key in order}
        for key in order:
            if key in SPLIT_LOADS:
                for i in range(CHUNK_TILES):
                    nc.sync.dma_start(out=chunk_raw[key][:, i, :], in_=chunks[key][0][:, i, :])
            else:
                nc.sync.dma_start(out=chunk_raw[key][:], in_=chunks[key][0])
            if key == ("x", 1):
                with nc.allow_non_contiguous_dma(reason="8 bytes of b2 to a partition and pass"):
                    nc.sync.dma_start(out=b2_bf[:], in_=b2_cols)
        wm_raw = raw.tile([P, K], BF16)
        wv_raw = raw.tile([P, K], BF16)
        eps_raw = raw.tile([P, ROW_TILES, C], BF16)
        nc.sync.dma_start(out=wm_raw[:], in_=Wm)
        nc.sync.dma_start(out=wv_raw[:], in_=Wv)
        nc.sync.dma_start(out=eps_raw[:], in_=eps_rows)
        gm_bf = const.tile([P, 1], BF16)
        gv_bf = const.tile([P, 1], BF16)
        betam_bf = const.tile([P, 1], BF16)
        betav_bf = const.tile([P, 1], BF16)
        with nc.allow_non_contiguous_dma(reason="one element of a norm's vector to a partition"):
            nc.sync.dma_start(out=gm_bf[:], in_=gm.rearrange("(p o) -> p o", o=1))
            nc.sync.dma_start(out=gv_bf[:], in_=gv.rearrange("(p o) -> p o", o=1))
            nc.sync.dma_start(out=betam_bf[:], in_=betam.rearrange("(p o) -> p o", o=1))
            nc.sync.dma_start(out=betav_bf[:], in_=betav.rearrange("(p o) -> p o", o=1))

        zeros = const.tile([P, CHUNK], BF16)
        nc.vector.memset(zeros[:], 0.0)
        ident_f32 = const.tile([P, P], F32)
        masks.make_identity(nc, ident_f32[:])
        one = const.tile([P, 1], F32)
        nc.vector.memset(one[:], 1.0)
        neg_half = const.tile([P, 1], F32)
        nc.vector.memset(neg_half[:], -0.5)

        grouped = {}
        acc = {}

        def flip(key, tiles=range(CHUNK_TILES), on_scalar=(1,)):
            whole = len(tiles) == CHUNK_TILES
            if whole:
                grouped[key] = stage.tile([P, PASSES * CHUNK * PACK], BF16, tag="grouped", name="grouped_%s%d" % key, align_bytes=64)
            for i in tiles:
                if not whole:
                    grouped[key, i] = stage.tile([P, PASSES * P * PACK], BF16, tag="grouped_tile", name="grouped_%s%d_%d" % (key + (i,)), align_bytes=64)
                grouped_words = (grouped[key] if whole else grouped[key, i])[:].bitcast(F32).rearrange("p (g r u) -> p g r u", g=PASSES, u=PAIRS)
                words = chunk_raw[key][:, i, :].bitcast(F32)
                flipped = flip_psum.tile([P, PASSES, PAIRS, P], F32, tag="flip")
                for g in range(PASSES):
                    for u in range(PAIRS):
                        block = g * PAIRS + u
                        nc.tensor.transpose(flipped[:, g, u, :], words[:, block * P : (block + 1) * P], ident_f32[:])
                dst = grouped_words[:, :, i * P : (i + 1) * P, :] if whole else grouped_words
                src = flipped[:].rearrange("p g u r -> p g r u")
                if i in on_scalar:
                    nc.scalar.copy(out=dst, in_=src)
                else:
                    nc.vector.tensor_copy(out=dst, in_=src)

        def quantise(key, tile=None):
            codes, scales = chunks[key][1], chunks[key][2]
            cols = slice(0, CHUNK) if tile is None else slice(tile * P, (tile + 1) * P)
            source = grouped[key] if tile is None else grouped[key, tile]
            if key[0] == "w" and tile is None:
                nc.vector.quantize_mx(
                    out=codes.rearrange("p g m -> p (g m)").bitcast(FP8X4), scales=scales.rearrange("p g m -> p (g m)"), in_=source[:]
                )
                return
            width = (cols.stop - cols.start) * PACK
            for g in range(PASSES):
                nc.vector.quantize_mx(
                    out=codes[:, g, cols].bitcast(FP8X4), scales=scales[:, g, cols], in_=source[:, g * width : (g + 1) * width]
                )

        def multiply(c, h, cols=slice(0, HALF), tiles=range(CHUNK_TILES)):
            for i in tiles:
                if (c, h, i) not in acc:
                    acc[c, h, i] = acc_psum.tile([P, HALF], F32, tag="acc", name="acc%d%d%d" % (c, h, i))
                m_cols = slice(i * P, (i + 1) * P)
                for g in range(PASSES):
                    nc.tensor.matmul_mx(
                        out=acc[c, h, i][:, cols],
                        lhsT=w_codes[c][:, g, m_cols].bitcast(FP8X4),
                        lhsT_scale=w_scales[c][:, g, m_cols],
                        rhs=x_codes[h][:, g, cols].bitcast(FP8X4),
                        rhs_scale=x_scales[h][:, g, cols],
                        start=(g == 0),
                        stop=(g == PASSES - 1),
                    )

        def exponentials(c, h, cols=slice(0, HALF)):
            for i in range(CHUNK_TILES):
                m = c * CHUNK_TILES + i
                g, t = divmod(m, PACK)
                nc.scalar.activation(out=exp_v[h][:, m, cols], in_=acc[c, h, i][:, cols], func=ACT.Exp, bias=b2_bf[:, g, t : t + 1], scale=1.0)

        head_idle = acc_psum.tile([P, HALF], F32, tag="acc", name="head_idle")

        def idle_matmuls(count):
            for n in range(count):
                nc.tensor.matmul(head_idle[:, :CHUNK], lhsT=zeros[:, :P], rhs=zeros[:], start=True, stop=True)

        idle_matmuls(HEAD_MATMULS)
        flip(("x", 0), (0,))
        quantise(("x", 0), 0)
        flip(("x", 0), (1,))
        idle_matmuls(2)
        flip(("w", 0), (0,))
        quantise(("x", 0), 1)
        quantise(("w", 0), 0)
        flip(("w", 0), (1,))
        idle_matmuls(2)
        quantise(("w", 0), 1)
        flip(("x", 1), (0,), on_scalar=(0,))
        flip(("x", 1), (1,), on_scalar=())
        multiply(0, 0, slice(0, CHUNK))
        exponentials(0, 0, slice(0, CHUNK))
        quantise(("x", 1), 0)
        quantise(("x", 1), 1)
        flip(("w", 1))
        quantise(("w", 1))
        flip(("w", 2))
        multiply(0, 0, slice(CHUNK, HALF))
        exponentials(0, 0, slice(CHUNK, HALF))
        flip(("w", 3))
        quantise(("w", 2))
        multiply(1, 0)
        exponentials(1, 0)
        flip(("x", 2))
        flip(("x", 3))
        quantise(("w", 3))
        multiply(2, 0)
        exponentials(2, 0)
        quantise(("x", 2))
        quantise(("x", 3))
        multiply(3, 0)
        exponentials(3, 0)
        for c in range(CHUNKS):
            multiply(c, 1)
            exponentials(c, 1)

        head_grouped = keep.tile([P, HEADS * PASSES * C * PACK], BF16, align_bytes=64)
        head_words = head_grouped[:].bitcast(F32).rearrange("p (s g c u) -> p s g c u", s=HEADS, g=PASSES, u=PAIRS)
        head_codes = keep.tile([P, HEADS, PASSES, C], U32, align_bytes=64)
        head_scales = keep.tile([P, HEADS, PASSES, C], U8, align_bytes=64)
        for s, rows in ((MEAN, wm_raw), (LOGVAR, wv_raw)):
            words = rows[:].bitcast(F32)
            flipped = flip_psum.tile([P, PASSES, PAIRS, P], F32, tag="flip")
            for g in range(PASSES):
                for u in range(PAIRS):
                    first = g * PAIRS * P + u
                    nc.tensor.transpose(flipped[:, g, u, :], words[:, first : (g + 1) * PAIRS * P : PAIRS], ident_f32[:])
            nc.vector.tensor_copy(out=head_words[:, s, :, :, :], in_=flipped[:].rearrange("p g u c -> p g c u"))
        nc.vector.quantize_mx(
            out=head_codes[:].rearrange("p s g c -> p (s g c)").bitcast(FP8X4),
            scales=head_scales[:].rearrange("p s g c -> p (s g c)"),
            in_=head_grouped[:],
        )

        gamma = const.tile([P, HEADS], F32)
        beta = const.tile([P, HEADS], F32)
        nc.vector.tensor_copy(out=gamma[:, MEAN : MEAN + 1], in_=gm_bf[:])
        nc.vector.tensor_copy(out=beta[:, MEAN : MEAN + 1], in_=betam_bf[:])
        nc.vector.tensor_scalar(out=gamma[:, LOGVAR : LOGVAR + 1], in0=gv_bf[:], scalar1=0.5, scalar2=None, op0=ALU.mult)
        nc.vector.tensor_scalar(out=beta[:, LOGVAR : LOGVAR + 1], in0=betav_bf[:], scalar1=0.5, scalar2=None, op0=ALU.mult)

        hidden = [[acc_psum.tile([P, HALF], F32, tag="acc", name="hidden%d%d" % (s, h)) for h in range(HALVES)] for s in range(HEADS)]
        stats = keep.tile([P, HEADS, len(EN2_PIECES), BN_STATS_DIM], F32)
        table_scratch = const.tile([P, 1], F32)

        def statistics(n, s):
            h, cols = half_of(EN2_PIECES[n])
            nc.vector.bn_stats(out=stats[:, s, n, :], in_=hidden[s][h][:, cols])

        idle = flip_psum.tile([P, HALF], F32, tag="flip")

        def idle_passes(count):
            for n in range(count):
                nc.tensor.matmul_mx(
                    out=idle[:],
                    lhsT=head_codes[:, MEAN, 0, :].bitcast(FP8X4),
                    lhsT_scale=head_scales[:, MEAN, 0, :],
                    rhs=x_codes[0][:, 0, :].bitcast(FP8X4),
                    rhs_scale=x_scales[0][:, 0, :],
                    start=True,
                    stop=True,
                )

        for n in range(len(EN2_PIECES)):
            h, cols = half_of(EN2_PIECES[n])
            width = EN2_PIECES[n][1]
            for g in range(PASSES):
                en2 = stage.tile([P, CHUNK * PACK], BF16, tag="en2", align_bytes=64)
                en2_codes = stage.tile([P, CHUNK], U32, tag="en2_codes", align_bytes=64)
                en2_scales = stage.tile([P, CHUNK], U8, tag="en2_scales", align_bytes=64)
                last = n == len(EN2_PIECES) - 1 and g == PASSES - 1
                step = width // 2 if last else width
                for first in range(0, width, step):
                    part = slice(first, first + step)
                    part_values = en2[:, first * PACK : (first + step) * PACK]
                    part_cols = slice(cols.start + first, cols.start + first + step)
                    nc.scalar.activation(
                        out=part_values.rearrange("p (a i t) -> p a t i", i=RUN, t=PACK),
                        in_=exp_v[h][:, g * PACK : (g + 1) * PACK, part_cols].rearrange("p t (a i) -> p a t i", i=RUN),
                        func=ACT.Ln,
                        bias=one[:],
                        scale=1.0,
                    )
                    if n > 0 and g == 0:
                        statistics(n - 1, LOGVAR)
                    nc.vector.quantize_mx(out=en2_codes[:, part].bitcast(FP8X4), scales=en2_scales[:, part], in_=part_values)
                if n > 0 and g == 0:
                    statistics(n - 1, MEAN)
                for s in (LOGVAR, MEAN):
                    nc.tensor.matmul_mx(
                        out=hidden[s][h][:, cols],
                        lhsT=head_codes[:, s, g, :].bitcast(FP8X4),
                        lhsT_scale=head_scales[:, s, g, :],
                        rhs=en2_codes[:, :width].bitcast(FP8X4),
                        rhs_scale=en2_scales[:, :width],
                        start=(g == 0),
                        stop=(g == PASSES - 1),
                    )
            if n == 1:
                even_spread = stats[:, :, 0, 2:3]
                nc.vector.tensor_scalar(out=even_spread, in0=even_spread, scalar1=ROWS * BN_EPS, scalar2=None, op0=ALU.add)
        nc.scalar.activation(out=table_scratch[:], in_=en2[:, 0:1], func=ACT.Exp)

        rstd = [const.tile([P, 1], F32, name="rstd%d" % s) for s in range(HEADS)]
        mean_var = const.tile([P, HEADS, BN_AGGR_DIM], F32)
        neg_mean_gamma = const.tile([P, HEADS], F32)
        gain = const.tile([P, HEADS], F32)
        shift = const.tile([P, HEADS], F32)
        for s in (LOGVAR, MEAN):
            col = slice(s, s + 1)
            statistics(len(EN2_PIECES) - 1, s)
            nc.vector.bn_aggr(out=mean_var[:, s, :], in_=stats[:, s, :, :].rearrange("p c k -> p (c k)"))
            nc.gpsimd.tensor_tensor(out=rstd[s][:], in0=mean_var[:, s, 1:2], in1=neg_half[:], op=ALU.pow)
            nc.vector.scalar_tensor_tensor(
                out=neg_mean_gamma[:, col], in0=mean_var[:, s, 0:1], scalar=-1.0, in1=gamma[:, col], op0=ALU.mult, op1=ALU.mult
            )
        for s in (LOGVAR, MEAN):
            col = slice(s, s + 1)
            nc.vector.tensor_tensor(out=gain[:, col], in0=rstd[s][:], in1=gamma[:, col], op=ALU.mult)
            nc.vector.tensor_scalar(
                out=shift[:, col], in0=neg_mean_gamma[:, col], scalar1=rstd[s][:], scalar2=beta[:, col], op0=ALU.mult, op1=ALU.add
            )

        idle_passes(TAIL_PASSES)

        pieces = range(len(Z_PIECES))
        std = [tail.tile([P, Z_PIECES[n][1]], F32, name="std%d" % n) for n in pieces]
        mean = [tail.tile([P, Z_PIECES[n][1]], F32, name="mean%d" % n) for n in pieces]
        noise = keep.tile([P, ROW_TILES, C], F32)
        z_rows = keep.tile([P, ROW_TILES, C], F32)

        def affine_flipped(n, s, func, columns):
            h, cols = half_of(Z_PIECES[n])
            col = slice(s, s + 1)
            nc.scalar.activation(out=columns[:], in_=hidden[s][h][:, cols], func=func, bias=shift[:, col], scale=gain[:, col])
            row_tiles = Z_PIECES[n][1] // P
            rows = flip_psum.tile([P, row_tiles, C], F32, tag="flip", name="rows%d%d" % (s, n))
            for i in range(row_tiles):
                nc.tensor.transpose(rows[:, i, :], columns[:, i * P : (i + 1) * P], ident_f32[:])
            return rows

        def tiles_of(n):
            first, width = Z_PIECES[n]
            return slice(first // P, (first + width) // P)

        def make_noise(n):
            std_rows = affine_flipped(n, LOGVAR, ACT.Exp, std[n])
            nc.vector.tensor_tensor(out=noise[:, tiles_of(n), :], in0=std_rows[:], in1=eps_raw[:, tiles_of(n), :], op=ALU.mult)

        def make_sample(n):
            mean_rows = affine_flipped(n, MEAN, ACT.Identity, mean[n])
            nc.vector.tensor_tensor(out=z_rows[:, tiles_of(n), :], in0=mean_rows[:], in1=noise[:, tiles_of(n), :], op=ALU.add)
            nc.sync.dma_start(out=out_rows[:, tiles_of(n), :], in_=z_rows[:, tiles_of(n), :])

        make_noise(0)
        for n in pieces[1:]:
            make_noise(n)
            make_sample(n - 1)
        make_sample(len(Z_PIECES) - 1)
